import numpy as np
import ml_dtypes


def mxq(x, axis, fmt="e4m3"):
    dtype, down = {"e4m3": (ml_dtypes.float8_e4m3fn, 7), "e5m2": (ml_dtypes.float8_e5m2, 14)}[fmt]
    v = np.moveaxis(np.asarray(x, np.float32).astype(ml_dtypes.bfloat16).astype(np.float64), axis, -1)
    blocks = v.reshape(v.shape[:-1] + (-1, 32))
    amax = np.abs(blocks).max(-1, keepdims=True)
    byte = np.maximum(np.where(amax > 0, np.frexp(amax)[1] - 1 + 127, 0) - down, 1)
    scale = np.exp2(byte - 127.0)
    codes = (blocks / scale).astype(np.float32).astype(dtype).astype(np.float64)
    return np.moveaxis((codes * scale).reshape(v.shape), -1, axis)


WIDE = False


def mx_kscale(k):
    if not WIDE:
        return np.ones(k)
    levels = np.array([10, -10, 5, -5, 0])
    a = np.random.permutation(np.resize(levels, k // 512 * 4)).reshape(k // 512, 4)
    idx = np.arange(k)
    return np.exp2(a[idx // 512, idx % 128 // 32])


BF16 = ml_dtypes.bfloat16


def bf(x):
    return np.asarray(x, np.float32).astype(BF16)


def f64(x):
    return np.asarray(x).astype(np.float64)


E2M1 = np.array([0.0, 0.5, 1.0, 1.5, 2.0, 3.0, 4.0, 6.0, -0.0, -0.5, -1.0, -1.5, -2.0, -3.0, -4.0, -6.0])


def pack_weight(w, fmt):
    k, n = w.shape
    w = f64(bf(w)).reshape(k // 32, 32, n)
    amax = np.abs(w).max(1)
    if fmt == "e4m3":
        byte = np.frexp(amax)[1] - 1 + 127 - 7
    else:
        mant, ex = np.frexp(amax / 6.0)
        byte = np.where(mant > 0.5, ex, ex - 1) + 127
    byte = np.clip(np.where(amax > 0, byte, 1), 1, 254)
    scaled = (w * np.exp2(127.0 - byte)[:, None, :]).reshape(k, n).astype(np.float32)
    by_word = np.ascontiguousarray(scaled.reshape(k // 512, 128, 4, n).transpose(0, 1, 3, 2))
    if fmt == "e4m3":
        words = by_word.astype(ml_dtypes.float8_e4m3fn).view(np.uint8)
    else:
        c = by_word.astype(ml_dtypes.float4_e2m1fn).view(np.uint8) & 0xF
        words = c[..., 0::2] | (c[..., 1::2] << 4)
    return np.ascontiguousarray(words), np.ascontiguousarray(byte.astype(np.uint8).reshape(k // 512, 16, n))


def unpack_weight(words, scales, fmt):
    g, p, n, _ = words.shape
    if fmt == "e4m3":
        vals = np.ascontiguousarray(words).view(ml_dtypes.float8_e4m3fn).astype(np.float64)
    else:
        nib = np.empty((g, p, n, 4), np.uint8)
        nib[..., 0::2] = words & 0xF
        nib[..., 1::2] = words >> 4
        vals = E2M1[nib]
    vals = vals * np.repeat(np.exp2(scales.astype(np.float64) - 127.0), 8, axis=1)[..., None]
    return vals.transpose(0, 1, 3, 2).reshape(g * 512, n)


B, S, D_MODEL, D_POS, H, D_FF = 512, 8, 512, 512, 4, 2048
DPP = D_POS // H
DPH = D_MODEL // H


def setup_inputs():
    s = mx_kscale(D_MODEL)
    gq = np.exp2(np.random.uniform(-1.0, 1.0, (S, H, B, 1)))
    gk = np.exp2(np.random.uniform(-1.0, 1.0, (S, H, B, 1)))
    q_pos = bf(np.random.standard_normal((S, H, B, DPP)) * gq * 3.0 / np.sqrt(DPP))
    k_pos = bf(np.random.standard_normal((S, H, B, DPP)) * gk * 3.0 / np.sqrt(DPP))
    x_grp = bf(np.random.standard_normal((S, B, D_MODEL)) * s)
    wv = np.random.standard_normal((D_MODEL, D_MODEL)) * 0.5 / np.sqrt(D_MODEL) / s
    words, scales = pack_weight(np.ascontiguousarray(wv.T), "e4m3")
    bv = bf(np.random.standard_normal(D_MODEL) * 10.0 / B)
    return {"q_pos": q_pos,
            "k_pos": k_pos,
            "x_grp": x_grp,
            "Wv_words": words,
            "Wv_scales": scales,
            "bv": bv}


def reference(q_pos, k_pos, x_grp, Wv_words, Wv_scales, bv):
    v = (mxq(f64(x_grp), 2, "e4m3") @ unpack_weight(Wv_words, Wv_scales, "e4m3")) + f64(bv)
    v = v.reshape(S, B, H, DPH).transpose(0, 2, 1, 3)
    q2 = np.sum(f64(q_pos) * f64(q_pos), axis=-1)
    k2 = np.sum(f64(k_pos) * f64(k_pos), axis=-1)
    d2 = q2[..., :, None] + k2[..., None, :] - 2.0 * (f64(q_pos) @ f64(k_pos).transpose(0, 1, 3, 2))
    dist = np.sqrt(np.maximum(d2, 1e-12)) + 1.0
    scores = 1.0 / dist
    causal = np.triu(np.ones((B, B), bool), k=1)
    scores = np.where(causal, 0.0, scores)
    o = mxq(scores, 3, "e4m3") @ mxq(v, 2, "e4m3")
    return o.transpose(0, 2, 1, 3).reshape(S, B, D_MODEL)

@@ -1,0 +1,309 @@
+from contextlib import ExitStack
+
+import concourse.mybir as mybir
+from concourse.masks import make_identity
+
+S, H, B, DM = 8, 4, 512, 512
+P = 128
+NT = B // P
+UNITS = S * H
+FLOPS = 3 * 2 * S * B * B * DM
+
+BF16 = mybir.dt.bfloat16
+F32 = mybir.dt.float32
+I32 = mybir.dt.int32
+U8 = mybir.dt.uint8
+U32 = mybir.dt.uint32
+FP8X4 = mybir.dt.float8_e4m3fn_x4
+ALU = mybir.AluOpType
+ACT = mybir.ActivationFunctionType
+
+PLANE_COLS = [B - t * P for t in range(NT)]
+PLANE_AT = [sum(PLANE_COLS[:t]) for t in range(NT)]
+LIVE = sum(PLANE_COLS)
+D2_FLOOR = 1e-12
+HUGE = 3.0e38
+
+TRANSPOSE_AHEAD = 3
+NORMS_AHEAD = 2
+Q2_AHEAD = 1
+ACT_BEHIND = 3
+WEIGHTS_BEHIND = 7
+ATTEND_BEHIND = 8
+
+
+def tile_networklayer_pb_t_kernel(tc, q_pos, k_pos, x_grp, Wv_words, Wv_scales, bv, out):
+    nc = tc.nc
+    with ExitStack() as ctx:
+        const = ctx.enter_context(tc.tile_pool(name="const", bufs=1))
+        rows = ctx.enter_context(tc.tile_pool(name="rows", bufs=2))
+        work = ctx.enter_context(tc.tile_pool(name="work", bufs=3))
+        ps_score = ctx.enter_context(tc.psum_pool(name="ps_score", bufs=3))
+        ps_prep = ctx.enter_context(tc.psum_pool(name="ps_prep", bufs=3))
+        ps_out = ctx.enter_context(tc.psum_pool(name="ps_out", bufs=2))
+        ctx.enter_context(tc.manual_schedule())
+
+        q_rows, k_rows, x_rows = {}, {}, {}
+        qk_t, q_sq, k2, k2_half, q2_half = {}, {}, {}, {}, {}
+        dist, grouped, w_codes, w_scl = {}, {}, {}, {}
+        x_codes, x_scl, v_grouped, v_codes, v_scl, o_sb = {}, {}, {}, {}, {}, {}
+
+        def load(g):
+            q_rows[g] = rows.tile([P, H * NT, P], BF16, name="q_rows", tag="q_rows")
+            nc.sync.dma_start(out=q_rows[g][:], in_=q_pos[g].rearrange("h (t p) d -> p (h t) d", p=P))
+            k_rows[g] = rows.tile([P, H * NT, P], BF16, name="k_rows", tag="k_rows")
+            nc.sync.dma_start(out=k_rows[g][:], in_=k_pos[g].rearrange("h (t p) d -> p (h t) d", p=P))
+            x_rows[g] = rows.tile([P, NT, DM], BF16, name="x_rows", tag="x_rows")
+            nc.sync.dma_start(out=x_rows[g][:], in_=x_grp[g].rearrange("(t p) k -> p t k", p=P))
+
+        load(0)
+
+        wv_words = const.tile([P, 4 * DM], U8, name="wv_words", align_bytes=64)
+        nc.sync.dma_start(
+            out=wv_words[:].bitcast(I32), in_=Wv_words[0].rearrange("p n t -> p (n t)").bitcast(I32)
+        )
+        wv_scl = const.tile([P, DM], U8, name="wv_scl", align_bytes=64)
+        nc.vector.memset(wv_scl[:].bitcast(I32), 0)
+        for quad in range(4):
+            nc.sync.dma_start(
+                out=wv_scl[32 * quad : 32 * quad + 4, :].bitcast(I32),
+                in_=Wv_scales[0, 4 * quad : 4 * quad + 4, :].bitcast(I32),
+            )
+        bias_bc = const.tile([P, DM], BF16, name="bias_bc")
+        nc.sync.dma_start(out=bias_bc[:], in_=bv.partition_broadcast(P))
+        load(1)
+
+        ident_bf = const.tile([P, P], BF16, name="ident_bf")
+        make_identity(nc, ident_bf[:])
+        ident_f32 = const.tile([P, P], F32, name="ident_f32")
+        make_identity(nc, ident_f32[:])
+        neg_half = const.tile([P, P], F32, name="neg_half")
+        nc.vector.memset(neg_half[:], -0.5)
+        keep_f32 = const.tile([P, P], F32, name="keep_f32")
+        nc.gpsimd.memset(keep_f32[:], 1.0)
+        nc.gpsimd.affine_select(
+            out=keep_f32[:],
+            in_=keep_f32[:],
+            pattern=[[1, P]],
+            compare_op=ALU.is_ge,
+            fill=0.0,
+            base=0,
+            channel_multiplier=-1,
+        )
+        keep = const.tile([P, P], BF16, name="keep")
+        nc.vector.tensor_copy(out=keep[:], in_=keep_f32[:])
+        squares_unused = const.tile([P, P], BF16, name="squares_unused")
+        w_planes = [const.tile([P, H, NT, B], BF16, name="w_planes%d" % i) for i in range(2)]
+        for planes in w_planes:
+            for t in range(1, NT):
+                nc.vector.memset(planes[:, :, t, : t * P], 0.0)
+
+        def transpose_qk(u):
+            g, h = divmod(u, H)
+            qk_ps = ps_prep.tile([P, 2 * B], BF16, name="qk_ps", tag="prep")
+            for t in range(NT):
+                nc.tensor.transpose(qk_ps[:, t * P : (t + 1) * P], q_rows[g][:, h * NT + t, :], ident_bf[:])
+            for t in range(NT):
+                nc.tensor.transpose(
+                    qk_ps[:, B + t * P : B + (t + 1) * P], k_rows[g][:, h * NT + t, :], ident_bf[:]
+                )
+            qk_t[u] = work.tile([P, 2 * B], BF16, name="qk_t", tag="qk_t", bufs=5)
+            nc.scalar.copy(out=qk_t[u][:], in_=qk_ps[:])
+
+        def norms(u):
+            g, h = divmod(u, H)
+            q_sq[u] = work.tile([P, B], F32, name="q_sq", tag="q_sq")
+            nc.gpsimd.tensor_tensor(out=q_sq[u][:], in0=qk_t[u][:, :B], in1=qk_t[u][:, :B], op=ALU.mult)
+            k2[u] = work.tile([P, NT], F32, name="k2", tag="k2", bufs=4)
+            for t in range(NT):
+                nc.scalar.activation(
+                    out=squares_unused[:],
+                    in_=k_rows[g][:, h * NT + t, :],
+                    func=ACT.Square,
+                    accum_out=k2[u][:, t : t + 1],
+                )
+
+        def q2_broadcast(u):
+            q2_ps = ps_prep.tile([P, B], F32, name="q2_ps", tag="prep")
+            nc.tensor.matmul(q2_ps[:], lhsT=neg_half[:], rhs=q_sq[u][:], start=True, stop=True)
+            q2_half[u] = work.tile([P, B], F32, name="q2_half", tag="q2_half")
+            nc.scalar.copy(out=q2_half[u][:], in_=q2_ps[:])
+            k2_half[u] = work.tile([P, NT], F32, name="k2_half", tag="k2_half", bufs=4)
+            nc.vector.tensor_scalar_mul(out=k2_half[u][:], in0=k2[u][:], scalar1=-0.5)
+
+        def scores(u):
+            g, h = divmod(u, H)
+            if h == 0:
+                dist[g] = work.tile([P, H, LIVE], F32, name="dist", tag="dist")
+            for t in range(NT):
+                n = PLANE_COLS[t]
+                kq_ps = ps_score.tile([P, B], F32, name="kq_ps", tag="kq")
+                nc.tensor.matmul(
+                    kq_ps[:, :n],
+                    lhsT=qk_t[u][:, B + t * P : B + (t + 1) * P],
+                    rhs=qk_t[u][:, t * P : B],
+                    start=True,
+                    stop=True,
+                )
+                nc.vector.scalar_tensor_tensor(
+                    out=dist[g][:, h, PLANE_AT[t] : PLANE_AT[t] + n],
+                    in0=kq_ps[:, :n],
+                    scalar=k2_half[u][:, t : t + 1],
+                    in1=q2_half[u][:, t * P : B],
+                    op0=ALU.add,
+                    op1=ALU.add,
+                )
+            nc.gpsimd.tensor_scalar(
+                out=dist[g][:, h, :],
+                in0=dist[g][:, h, :],
+                scalar1=-0.5 * D2_FLOOR,
+                scalar2=-HUGE,
+                op0=ALU.min,
+                op1=ALU.max,
+            )
+
+        def activations(step):
+            g, quarter = divmod(step, 4)
+            if quarter < 2:
+                two_heads = dist[g][:, 2 * quarter : 2 * quarter + 2, :]
+                nc.scalar.activation(out=two_heads, in_=two_heads, func=ACT.Ln, scale=-2.0)
+            else:
+                for t in (0, 3) if quarter == 2 else (1, 2):
+                    nc.scalar.activation(
+                        out=w_planes[g % 2][:, :, t, t * P :],
+                        in_=dist[g][:, :, PLANE_AT[t] : PLANE_AT[t] + PLANE_COLS[t]],
+                        func=ACT.Sigmoid,
+                        scale=-0.5,
+                    )
+
+        def mask_diagonal(g):
+            for t in range(NT):
+                block = w_planes[g % 2][:, :, t, t * P : (t + 1) * P]
+                nc.vector.tensor_tensor(
+                    out=block, in0=block, in1=keep[:].unsqueeze(1).to_broadcast([P, H, P]), op=ALU.mult
+                )
+
+        def regroup_w(u):
+            g, h = divmod(u, H)
+            grouped[u] = work.tile([P, B, NT], BF16, name="grouped", tag="grouped", bufs=2, align_bytes=64)
+            nc.vector.tensor_copy(
+                out=grouped[u][:].rearrange("p (c i) t -> p c t i", i=4),
+                in_=w_planes[g % 2][:, h, :, :].rearrange("p t (c i) -> p c t i", i=4),
+            )
+
+        def quantise_w(u):
+            w_codes[u] = work.tile([P, B], U32, name="w_codes", tag="w_codes", align_bytes=64)
+            w_scl[u] = work.tile([P, B], U8, name="w_scl", tag="w_scl", align_bytes=64)
+            nc.vector.quantize_mx(
+                out=w_codes[u][:].bitcast(FP8X4),
+                scales=w_scl[u][:],
+                in_=grouped[u][:].rearrange("p b t -> p (b t)"),
+            )
+
+        def attend(u):
+            g, h = divmod(u, H)
+            o_ps = ps_out.tile([P, NT, P], F32, name="o_ps", tag="o")
+            for i in range(NT):
+                nc.tensor.matmul_mx(
+                    out=o_ps[:, i, :],
+                    lhsT=w_codes[u][:, i * P : (i + 1) * P].bitcast(FP8X4),
+                    lhsT_scale=w_scl[u][:, i * P : (i + 1) * P],
+                    rhs=v_codes[g][:, h * P : (h + 1) * P].bitcast(FP8X4),
+                    rhs_scale=v_scl[g][:, h * P : (h + 1) * P],
+                    start=True,
+                    stop=True,
+                )
+            if h == 0:
+                o_sb[g] = work.tile([P, NT, DM], F32, name="o_sb", tag="o_sb", bufs=2)
+            nc.vector.tensor_copy(out=o_sb[g][:, :, h * P : (h + 1) * P], in_=o_ps[:])
+            if h == H - 1:
+                nc.sync.dma_start(out=out[g].rearrange("(i p) n -> p i n", p=P), in_=o_sb[g][:])
+
+        def transpose_x(g):
+            x_grouped = work.tile([P, NT, P, 4], BF16, name="x_grouped", tag="x_grouped", bufs=2, align_bytes=64)
+            for pair in range(NT // 2):
+                x_ps = ps_prep.tile([P, 2, 2, P], F32, name="x_ps", tag="prep")
+                for j in range(2):
+                    words = x_rows[g][:, 2 * pair + j, :].bitcast(F32)
+                    for u in range(2):
+                        nc.tensor.transpose(x_ps[:, j, u, :], words[:, u : DM // 2 : 2], ident_f32[:])
+                nc.vector.tensor_copy(
+                    out=x_grouped[:].bitcast(F32)[:, 2 * pair : 2 * pair + 2, :, :],
+                    in_=x_ps[:].rearrange("p j u c -> p j c u"),
+                )
+            return x_grouped
+
+        def quantise_x(g, x_grouped):
+            x_codes[g] = work.tile([P, B], U32, name="x_codes", tag="x_codes", bufs=2, align_bytes=64)
+            x_scl[g] = work.tile([P, B], U8, name="x_scl", tag="x_scl", bufs=2, align_bytes=64)
+            nc.vector.quantize_mx(
+                out=x_codes[g][:].bitcast(FP8X4),
+                scales=x_scl[g][:],
+                in_=x_grouped[:].rearrange("p t c v -> p (t c v)"),
+            )
+
+        def project_values(u):
+            g, h = divmod(u, H)
+            v_ps = ps_prep.tile([P, NT, P], F32, name="v_ps", tag="prep")
+            for t in range(NT):
+                nc.tensor.matmul_mx(
+                    out=v_ps[:, t, :],
+                    lhsT=x_codes[g][:, t * P : (t + 1) * P].bitcast(FP8X4),
+                    lhsT_scale=x_scl[g][:, t * P : (t + 1) * P],
+                    rhs=wv_words[:, 4 * h * P : 4 * (h + 1) * P].bitcast(FP8X4),
+                    rhs_scale=wv_scl[:, h * P : (h + 1) * P],
+                    start=True,
+                    stop=True,
+                )
+            if h == 0:
+                v_grouped[g] = work.tile([P, DM, NT], BF16, name="v_grouped", tag="v_grouped", bufs=2, align_bytes=64)
+            nc.vector.tensor_tensor(
+                out=v_grouped[g][:, h * P : (h + 1) * P, :],
+                in0=v_ps[:].rearrange("p t n -> p n t"),
+                in1=bias_bc[:, h * P : (h + 1) * P].unsqueeze(2).to_broadcast([P, P, NT]),
+                op=ALU.add,
+            )
+
+        def quantise_v(g):
+            v_codes[g] = work.tile([P, DM], U32, name="v_codes", tag="v_codes", align_bytes=64)
+            v_scl[g] = work.tile([P, DM], U8, name="v_scl", tag="v_scl", align_bytes=64)
+            nc.vector.quantize_mx(
+                out=v_codes[g][:].bitcast(FP8X4),
+                scales=v_scl[g][:],
+                in_=v_grouped[g][:].rearrange("p n t -> p (n t)"),
+            )
+
+        def is_unit(u):
+            return 0 <= u < UNITS
+
+        x_waiting = {}
+        for tick in range(-TRANSPOSE_AHEAD, UNITS + ATTEND_BEHIND):
+            if is_unit(tick - ACT_BEHIND):
+                activations(tick - ACT_BEHIND)
+            if is_unit(tick - WEIGHTS_BEHIND):
+                if (tick - WEIGHTS_BEHIND) % H == 0:
+                    mask_diagonal((tick - WEIGHTS_BEHIND) // H)
+                regroup_w(tick - WEIGHTS_BEHIND)
+            if is_unit(tick + NORMS_AHEAD):
+                norms(tick + NORMS_AHEAD)
+            if is_unit(tick):
+                scores(tick)
+            if is_unit(tick - WEIGHTS_BEHIND):
+                quantise_w(tick - WEIGHTS_BEHIND)
+            if is_unit(tick + Q2_AHEAD):
+                q2_broadcast(tick + Q2_AHEAD)
+            if is_unit(tick):
+                project_values(tick)
+            if is_unit(tick - H) and tick % H == 0:
+                quantise_v(tick // H - 1)
+            if is_unit(tick - ATTEND_BEHIND):
+                attend(tick - ATTEND_BEHIND)
+            if is_unit(tick + TRANSPOSE_AHEAD):
+                transpose_qk(tick + TRANSPOSE_AHEAD)
+            if is_unit(tick + 2) and (tick + 2) % H == 0:
+                x_waiting[(tick + 2) // H] = transpose_x((tick + 2) // H)
+            if is_unit(tick + 1) and (tick + 1) % H == 0:
+                quantise_x((tick + 1) // H, x_waiting[(tick + 1) // H])
+            if is_unit(tick + NORMS_AHEAD) and (tick + NORMS_AHEAD) % H == H - 1:
+                if (tick + NORMS_AHEAD) // H + 2 < S:
+                    load((tick + NORMS_AHEAD) // H + 2)

@@ -22,7 +22,6 @@ PLANE_COLS = [B - t * P for t in range(NT)]
 PLANE_AT = [sum(PLANE_COLS[:t]) for t in range(NT)]
 LIVE = sum(PLANE_COLS)
 D2_FLOOR = 1e-12
-HUGE = 3.0e38
 
 TRANSPOSE_AHEAD = 3
 NORMS_AHEAD = 2
@@ -123,11 +122,14 @@ def tile_networklayer_pb_t_kernel(tc, q_pos, k_pos, x_grp, Wv_words, Wv_scales, 
                     accum_out=k2[u][:, t : t + 1],
                 )
 
-        def q2_broadcast(u):
-            q2_ps = ps_prep.tile([P, B], F32, name="q2_ps", tag="prep")
-            nc.tensor.matmul(q2_ps[:], lhsT=neg_half[:], rhs=q_sq[u][:], start=True, stop=True)
-            q2_half[u] = work.tile([P, B], F32, name="q2_half", tag="q2_half")
-            nc.scalar.copy(out=q2_half[u][:], in_=q2_ps[:])
+        def half_norms(u):
+            q2_ps = ps_prep.tile([P, NT, 2], F32, name="q2_ps", tag="prep")
+            for i in range(NT):
+                nc.tensor.matmul(
+                    q2_ps[:, i, :], lhsT=q_sq[u][:, i * P : (i + 1) * P], rhs=neg_half[:, 0:2], start=True, stop=True
+                )
+            q2_half[u] = work.tile([P, NT, 2], F32, name="q2_half", tag="q2_half", bufs=4)
+            nc.vector.tensor_copy(out=q2_half[u][:], in_=q2_ps[:])
             k2_half[u] = work.tile([P, NT], F32, name="k2_half", tag="k2_half", bufs=4)
             nc.vector.tensor_scalar_mul(out=k2_half[u][:], in0=k2[u][:], scalar1=-0.5)
 
@@ -143,24 +145,25 @@ def tile_networklayer_pb_t_kernel(tc, q_pos, k_pos, x_grp, Wv_words, Wv_scales, 
                     lhsT=qk_t[u][:, B + t * P : B + (t + 1) * P],
                     rhs=qk_t[u][:, t * P : B],
                     start=True,
-                    stop=True,
+                    stop=False,
                 )
-                nc.vector.scalar_tensor_tensor(
+                for i in range(t, NT):
+                    nc.tensor.matmul(
+                        kq_ps[:, (i - t) * P : (i - t + 1) * P],
+                        lhsT=q2_half[u][:, i, 0:1].to_broadcast([P, P]),
+                        rhs=ident_f32[:],
+                        is_transpose=True,
+                        start=False,
+                        stop=(i == NT - 1),
+                    )
+                nc.vector.tensor_scalar(
                     out=dist[g][:, h, PLANE_AT[t] : PLANE_AT[t] + n],
                     in0=kq_ps[:, :n],
-                    scalar=k2_half[u][:, t : t + 1],
-                    in1=q2_half[u][:, t * P : B],
+                    scalar1=k2_half[u][:, t : t + 1],
+                    scalar2=-0.5 * D2_FLOOR,
                     op0=ALU.add,
-                    op1=ALU.add,
+                    op1=ALU.min,
                 )
-            nc.gpsimd.tensor_scalar(
-                out=dist[g][:, h, :],
-                in0=dist[g][:, h, :],
-                scalar1=-0.5 * D2_FLOOR,
-                scalar2=-HUGE,
-                op0=ALU.min,
-                op1=ALU.max,
-            )
 
         def activations(step):
             g, quarter = divmod(step, 4)
@@ -215,7 +218,10 @@ def tile_networklayer_pb_t_kernel(tc, q_pos, k_pos, x_grp, Wv_words, Wv_scales, 
                 )
             if h == 0:
                 o_sb[g] = work.tile([P, NT, DM], F32, name="o_sb", tag="o_sb", bufs=2)
-            nc.vector.tensor_copy(out=o_sb[g][:, :, h * P : (h + 1) * P], in_=o_ps[:])
+            if u % 2 == 0:
+                nc.scalar.copy(out=o_sb[g][:, :, h * P : (h + 1) * P], in_=o_ps[:])
+            else:
+                nc.vector.tensor_copy(out=o_sb[g][:, :, h * P : (h + 1) * P], in_=o_ps[:])
             if h == H - 1:
                 nc.sync.dma_start(out=out[g].rearrange("(i p) n -> p i n", p=P), in_=o_sb[g][:])
 
@@ -291,7 +297,7 @@ def tile_networklayer_pb_t_kernel(tc, q_pos, k_pos, x_grp, Wv_words, Wv_scales, 
             if is_unit(tick - WEIGHTS_BEHIND):
                 quantise_w(tick - WEIGHTS_BEHIND)
             if is_unit(tick + Q2_AHEAD):
-                q2_broadcast(tick + Q2_AHEAD)
+                half_norms(tick + Q2_AHEAD)
             if is_unit(tick):
                 project_values(tick)
             if is_unit(tick - H) and tick % H == 0:

@@ -147,6 +147,14 @@ def tile_networklayer_pb_t_kernel(tc, q_pos, k_pos, x_grp, Wv_words, Wv_scales, 
                     start=True,
                     stop=False,
                 )
+                if t > 0:
+                    nc.tensor.matmul(
+                        kq_ps[:, n:],
+                        lhsT=qk_t[u][:, B + t * P : B + (t + 1) * P],
+                        rhs=qk_t[u][:, : t * P],
+                        start=False,
+                        stop=False,
+                    )
                 for i in range(t, NT):
                     nc.tensor.matmul(
                         kq_ps[:, (i - t) * P : (i - t + 1) * P],

@@ -43,7 +43,7 @@ def tile_networklayer_pb_t_kernel(tc, q_pos, k_pos, x_grp, Wv_words, Wv_scales, 
         ctx.enter_context(tc.manual_schedule())
 
         q_rows, k_rows, x_rows = {}, {}, {}
-        qk_t, q_sq, k2, k2_half, q2_half = {}, {}, {}, {}, {}
+        qk_t, qk_sq, half_norm = {}, {}, {}
         dist, grouped, w_codes, w_scl = {}, {}, {}, {}
         x_codes, x_scl, v_grouped, v_codes, v_scl, o_sb = {}, {}, {}, {}, {}, {}
 
@@ -91,7 +91,6 @@ def tile_networklayer_pb_t_kernel(tc, q_pos, k_pos, x_grp, Wv_words, Wv_scales, 
         )
         keep = const.tile([P, P], BF16, name="keep")
         nc.vector.tensor_copy(out=keep[:], in_=keep_f32[:])
-        squares_unused = const.tile([P, P], BF16, name="squares_unused")
         w_planes = [const.tile([P, H, NT, B], BF16, name="w_planes%d" % i) for i in range(2)]
         for planes in w_planes:
             for t in range(1, NT):
@@ -109,29 +108,18 @@ def tile_networklayer_pb_t_kernel(tc, q_pos, k_pos, x_grp, Wv_words, Wv_scales, 
             qk_t[u] = work.tile([P, 2 * B], BF16, name="qk_t", tag="qk_t", bufs=5)
             nc.scalar.copy(out=qk_t[u][:], in_=qk_ps[:])
 
-        def norms(u):
-            g, h = divmod(u, H)
-            q_sq[u] = work.tile([P, B], F32, name="q_sq", tag="q_sq")
-            nc.gpsimd.tensor_tensor(out=q_sq[u][:], in0=qk_t[u][:, :B], in1=qk_t[u][:, :B], op=ALU.mult)
-            k2[u] = work.tile([P, NT], F32, name="k2", tag="k2", bufs=4)
-            for t in range(NT):
-                nc.scalar.activation(
-                    out=squares_unused[:],
-                    in_=k_rows[g][:, h * NT + t, :],
-                    func=ACT.Square,
-                    accum_out=k2[u][:, t : t + 1],
-                )
+        def squares(u):
+            qk_sq[u] = work.tile([P, 2 * B], F32, name="qk_sq", tag="qk_sq")
+            nc.scalar.activation(out=qk_sq[u][:], in_=qk_t[u][:], func=ACT.Square)
 
         def half_norms(u):
-            q2_ps = ps_prep.tile([P, NT, 2], F32, name="q2_ps", tag="prep")
-            for i in range(NT):
+            norm_ps = ps_prep.tile([P, 2 * NT, 2], F32, name="norm_ps", tag="prep")
+            for i in range(2 * NT):
                 nc.tensor.matmul(
-                    q2_ps[:, i, :], lhsT=q_sq[u][:, i * P : (i + 1) * P], rhs=neg_half[:, 0:2], start=True, stop=True
+                    norm_ps[:, i, :], lhsT=qk_sq[u][:, i * P : (i + 1) * P], rhs=neg_half[:, 0:2], start=True, stop=True
                 )
-            q2_half[u] = work.tile([P, NT, 2], F32, name="q2_half", tag="q2_half", bufs=4)
-            nc.vector.tensor_copy(out=q2_half[u][:], in_=q2_ps[:])
-            k2_half[u] = work.tile([P, NT], F32, name="k2_half", tag="k2_half", bufs=4)
-            nc.vector.tensor_scalar_mul(out=k2_half[u][:], in0=k2[u][:], scalar1=-0.5)
+            half_norm[u] = work.tile([P, 2 * NT, 2], F32, name="half_norm", tag="half_norm", bufs=4)
+            nc.vector.tensor_copy(out=half_norm[u][:], in_=norm_ps[:])
 
         def scores(u):
             g, h = divmod(u, H)
@@ -147,18 +135,10 @@ def tile_networklayer_pb_t_kernel(tc, q_pos, k_pos, x_grp, Wv_words, Wv_scales, 
                     start=True,
                     stop=False,
                 )
-                if t > 0:
-                    nc.tensor.matmul(
-                        kq_ps[:, n:],
-                        lhsT=qk_t[u][:, B + t * P : B + (t + 1) * P],
-                        rhs=qk_t[u][:, : t * P],
-                        start=False,
-                        stop=False,
-                    )
                 for i in range(t, NT):
                     nc.tensor.matmul(
                         kq_ps[:, (i - t) * P : (i - t + 1) * P],
-                        lhsT=q2_half[u][:, i, 0:1].to_broadcast([P, P]),
+                        lhsT=half_norm[u][:, i, 0:1].to_broadcast([P, P]),
                         rhs=ident_f32[:],
                         is_transpose=True,
                         start=False,
@@ -167,7 +147,7 @@ def tile_networklayer_pb_t_kernel(tc, q_pos, k_pos, x_grp, Wv_words, Wv_scales, 
                 nc.vector.tensor_scalar(
                     out=dist[g][:, h, PLANE_AT[t] : PLANE_AT[t] + n],
                     in0=kq_ps[:, :n],
-                    scalar1=k2_half[u][:, t : t + 1],
+                    scalar1=half_norm[u][:, NT + t, 0:1],
                     scalar2=-0.5 * D2_FLOOR,
                     op0=ALU.add,
                     op1=ALU.min,
@@ -299,7 +279,7 @@ def tile_networklayer_pb_t_kernel(tc, q_pos, k_pos, x_grp, Wv_words, Wv_scales, 
                     mask_diagonal((tick - WEIGHTS_BEHIND) // H)
                 regroup_w(tick - WEIGHTS_BEHIND)
             if is_unit(tick + NORMS_AHEAD):
-                norms(tick + NORMS_AHEAD)
+                squares(tick + NORMS_AHEAD)
             if is_unit(tick):
                 scores(tick)
             if is_unit(tick - WEIGHTS_BEHIND):

@@ -37,15 +37,15 @@ def tile_networklayer_pb_t_kernel(tc, q_pos, k_pos, x_grp, Wv_words, Wv_scales, 
         const = ctx.enter_context(tc.tile_pool(name="const", bufs=1))
         rows = ctx.enter_context(tc.tile_pool(name="rows", bufs=2))
         work = ctx.enter_context(tc.tile_pool(name="work", bufs=3))
-        ps_score = ctx.enter_context(tc.psum_pool(name="ps_score", bufs=3))
+        ps_score = ctx.enter_context(tc.psum_pool(name="ps_score", bufs=NT))
         ps_prep = ctx.enter_context(tc.psum_pool(name="ps_prep", bufs=3))
-        ps_out = ctx.enter_context(tc.psum_pool(name="ps_out", bufs=2))
+        ps_out = ctx.enter_context(tc.psum_pool(name="ps_out", bufs=1))
         ctx.enter_context(tc.manual_schedule())
 
         q_rows, k_rows, x_rows = {}, {}, {}
-        qk_t, qk_sq, half_norm = {}, {}, {}
+        qk_t, q_sq, k2, k2_half, q2_half = {}, {}, {}, {}, {}
         dist, grouped, w_codes, w_scl = {}, {}, {}, {}
-        x_codes, x_scl, v_grouped, v_codes, v_scl, o_sb = {}, {}, {}, {}, {}, {}
+        x_codes, x_scl, v_grouped, v_codes, v_scl = {}, {}, {}, {}, {}
 
         def load(g):
             q_rows[g] = rows.tile([P, H * NT, P], BF16, name="q_rows", tag="q_rows")
@@ -78,6 +78,8 @@ def tile_networklayer_pb_t_kernel(tc, q_pos, k_pos, x_grp, Wv_words, Wv_scales, 
         make_identity(nc, ident_f32[:])
         neg_half = const.tile([P, P], F32, name="neg_half")
         nc.vector.memset(neg_half[:], -0.5)
+        table_warmer = const.tile([P, 1], F32, name="table_warmer")
+        nc.scalar.activation(out=table_warmer[:], in_=neg_half[:, 0:1], func=ACT.Ln, scale=-2.0)
         keep_f32 = const.tile([P, P], F32, name="keep_f32")
         nc.gpsimd.memset(keep_f32[:], 1.0)
         nc.gpsimd.affine_select(
@@ -91,6 +93,7 @@ def tile_networklayer_pb_t_kernel(tc, q_pos, k_pos, x_grp, Wv_words, Wv_scales, 
         )
         keep = const.tile([P, P], BF16, name="keep")
         nc.vector.tensor_copy(out=keep[:], in_=keep_f32[:])
+        squares_unused = const.tile([P, P], BF16, name="squares_unused")
         w_planes = [const.tile([P, H, NT, B], BF16, name="w_planes%d" % i) for i in range(2)]
         for planes in w_planes:
             for t in range(1, NT):
@@ -108,18 +111,29 @@ def tile_networklayer_pb_t_kernel(tc, q_pos, k_pos, x_grp, Wv_words, Wv_scales, 
             qk_t[u] = work.tile([P, 2 * B], BF16, name="qk_t", tag="qk_t", bufs=5)
             nc.scalar.copy(out=qk_t[u][:], in_=qk_ps[:])
 
-        def squares(u):
-            qk_sq[u] = work.tile([P, 2 * B], F32, name="qk_sq", tag="qk_sq")
-            nc.scalar.activation(out=qk_sq[u][:], in_=qk_t[u][:], func=ACT.Square)
+        def norms(u):
+            g, h = divmod(u, H)
+            q_sq[u] = work.tile([P, B], F32, name="q_sq", tag="q_sq")
+            nc.gpsimd.tensor_tensor(out=q_sq[u][:], in0=qk_t[u][:, :B], in1=qk_t[u][:, :B], op=ALU.mult)
+            k2[u] = work.tile([P, NT], F32, name="k2", tag="k2", bufs=4)
+            for t in range(NT):
+                nc.scalar.activation(
+                    out=squares_unused[:],
+                    in_=k_rows[g][:, h * NT + t, :],
+                    func=ACT.Square,
+                    accum_out=k2[u][:, t : t + 1],
+                )
 
         def half_norms(u):
-            norm_ps = ps_prep.tile([P, 2 * NT, 2], F32, name="norm_ps", tag="prep")
-            for i in range(2 * NT):
+            q2_ps = ps_prep.tile([P, NT, 2], F32, name="q2_ps", tag="prep")
+            for i in range(NT):
                 nc.tensor.matmul(
-                    norm_ps[:, i, :], lhsT=qk_sq[u][:, i * P : (i + 1) * P], rhs=neg_half[:, 0:2], start=True, stop=True
+                    q2_ps[:, i, :], lhsT=q_sq[u][:, i * P : (i + 1) * P], rhs=neg_half[:, 0:2], start=True, stop=True
                 )
-            half_norm[u] = work.tile([P, 2 * NT, 2], F32, name="half_norm", tag="half_norm", bufs=4)
-            nc.vector.tensor_copy(out=half_norm[u][:], in_=norm_ps[:])
+            q2_half[u] = work.tile([P, NT, 2], F32, name="q2_half", tag="q2_half", bufs=4)
+            nc.vector.tensor_copy(out=q2_half[u][:], in_=q2_ps[:])
+            k2_half[u] = work.tile([P, NT], F32, name="k2_half", tag="k2_half", bufs=4)
+            nc.vector.tensor_scalar_mul(out=k2_half[u][:], in0=k2[u][:], scalar1=-0.5)
 
         def scores(u):
             g, h = divmod(u, H)
@@ -138,7 +152,7 @@ def tile_networklayer_pb_t_kernel(tc, q_pos, k_pos, x_grp, Wv_words, Wv_scales, 
                 for i in range(t, NT):
                     nc.tensor.matmul(
                         kq_ps[:, (i - t) * P : (i - t + 1) * P],
-                        lhsT=half_norm[u][:, i, 0:1].to_broadcast([P, P]),
+                        lhsT=q2_half[u][:, i, 0:1].to_broadcast([P, P]),
                         rhs=ident_f32[:],
                         is_transpose=True,
                         start=False,
@@ -147,7 +161,7 @@ def tile_networklayer_pb_t_kernel(tc, q_pos, k_pos, x_grp, Wv_words, Wv_scales, 
                 nc.vector.tensor_scalar(
                     out=dist[g][:, h, PLANE_AT[t] : PLANE_AT[t] + n],
                     in0=kq_ps[:, :n],
-                    scalar1=half_norm[u][:, NT + t, 0:1],
+                    scalar1=k2_half[u][:, t : t + 1],
                     scalar2=-0.5 * D2_FLOOR,
                     op0=ALU.add,
                     op1=ALU.min,
@@ -204,14 +218,9 @@ def tile_networklayer_pb_t_kernel(tc, q_pos, k_pos, x_grp, Wv_words, Wv_scales, 
                     start=True,
                     stop=True,
                 )
-            if h == 0:
-                o_sb[g] = work.tile([P, NT, DM], F32, name="o_sb", tag="o_sb", bufs=2)
-            if u % 2 == 0:
-                nc.scalar.copy(out=o_sb[g][:, :, h * P : (h + 1) * P], in_=o_ps[:])
-            else:
-                nc.vector.tensor_copy(out=o_sb[g][:, :, h * P : (h + 1) * P], in_=o_ps[:])
-            if h == H - 1:
-                nc.sync.dma_start(out=out[g].rearrange("(i p) n -> p i n", p=P), in_=o_sb[g][:])
+            o_sb = work.tile([P, NT, P], F32, name="o_sb", tag="o_sb")
+            nc.scalar.copy(out=o_sb[:], in_=o_ps[:])
+            nc.sync.dma_start(out=out[g, :, h * P : (h + 1) * P].rearrange("(i p) n -> p i n", p=P), in_=o_sb[:])
 
         def transpose_x(g):
             x_grouped = work.tile([P, NT, P, 4], BF16, name="x_grouped", tag="x_grouped", bufs=2, align_bytes=64)
@@ -279,7 +288,7 @@ def tile_networklayer_pb_t_kernel(tc, q_pos, k_pos, x_grp, Wv_words, Wv_scales, 
                     mask_diagonal((tick - WEIGHTS_BEHIND) // H)
                 regroup_w(tick - WEIGHTS_BEHIND)
             if is_unit(tick + NORMS_AHEAD):
-                squares(tick + NORMS_AHEAD)
+                norms(tick + NORMS_AHEAD)
             if is_unit(tick):
                 scores(tick)
             if is_unit(tick - WEIGHTS_BEHIND):

@@ -131,9 +131,11 @@ def tile_networklayer_pb_t_kernel(tc, q_pos, k_pos, x_grp, Wv_words, Wv_scales, 
                     q2_ps[:, i, :], lhsT=q_sq[u][:, i * P : (i + 1) * P], rhs=neg_half[:, 0:2], start=True, stop=True
                 )
             q2_half[u] = work.tile([P, NT, 2], F32, name="q2_half", tag="q2_half", bufs=4)
-            nc.vector.tensor_copy(out=q2_half[u][:], in_=q2_ps[:])
+            nc.scalar.copy(out=q2_half[u][:], in_=q2_ps[:])
             k2_half[u] = work.tile([P, NT], F32, name="k2_half", tag="k2_half", bufs=4)
-            nc.vector.tensor_scalar_mul(out=k2_half[u][:], in0=k2[u][:], scalar1=-0.5)
+            nc.gpsimd.tensor_scalar(
+                out=k2_half[u][:], in0=k2[u][:], scalar1=-0.5, scalar2=0.0, op0=ALU.mult, op1=ALU.add
+            )
 
         def scores(u):
             g, h = divmod(u, H)
@@ -230,7 +232,7 @@ def tile_networklayer_pb_t_kernel(tc, q_pos, k_pos, x_grp, Wv_words, Wv_scales, 
                     words = x_rows[g][:, 2 * pair + j, :].bitcast(F32)
                     for u in range(2):
                         nc.tensor.transpose(x_ps[:, j, u, :], words[:, u : DM // 2 : 2], ident_f32[:])
-                nc.vector.tensor_copy(
+                nc.scalar.copy(
                     out=x_grouped[:].bitcast(F32)[:, 2 * pair : 2 * pair + 2, :, :],
                     in_=x_ps[:].rearrange("p j u c -> p j c u"),
                 )

@@ -27,8 +27,9 @@ TRANSPOSE_AHEAD = 3
 NORMS_AHEAD = 2
 Q2_AHEAD = 1
 ACT_BEHIND = 3
-WEIGHTS_BEHIND = 7
-ATTEND_BEHIND = 8
+MASK_BEHIND = 7
+WEIGHTS_BEHIND = 8
+ATTEND_BEHIND = 9
 
 
 def tile_networklayer_pb_t_kernel(tc, q_pos, k_pos, x_grp, Wv_words, Wv_scales, bv, out):
@@ -109,7 +110,7 @@ def tile_networklayer_pb_t_kernel(tc, q_pos, k_pos, x_grp, Wv_words, Wv_scales, 
                     qk_ps[:, B + t * P : B + (t + 1) * P], k_rows[g][:, h * NT + t, :], ident_bf[:]
                 )
             qk_t[u] = work.tile([P, 2 * B], BF16, name="qk_t", tag="qk_t", bufs=5)
-            nc.scalar.copy(out=qk_t[u][:], in_=qk_ps[:])
+            nc.vector.tensor_copy(out=qk_t[u][:], in_=qk_ps[:])
 
         def norms(u):
             g, h = divmod(u, H)
@@ -131,7 +132,7 @@ def tile_networklayer_pb_t_kernel(tc, q_pos, k_pos, x_grp, Wv_words, Wv_scales, 
                     q2_ps[:, i, :], lhsT=q_sq[u][:, i * P : (i + 1) * P], rhs=neg_half[:, 0:2], start=True, stop=True
                 )
             q2_half[u] = work.tile([P, NT, 2], F32, name="q2_half", tag="q2_half", bufs=4)
-            nc.scalar.copy(out=q2_half[u][:], in_=q2_ps[:])
+            nc.vector.tensor_copy(out=q2_half[u][:], in_=q2_ps[:])
             k2_half[u] = work.tile([P, NT], F32, name="k2_half", tag="k2_half", bufs=4)
             nc.gpsimd.tensor_scalar(
                 out=k2_half[u][:], in0=k2[u][:], scalar1=-0.5, scalar2=0.0, op0=ALU.mult, op1=ALU.add
@@ -186,7 +187,7 @@ def tile_networklayer_pb_t_kernel(tc, q_pos, k_pos, x_grp, Wv_words, Wv_scales, 
         def mask_diagonal(g):
             for t in range(NT):
                 block = w_planes[g % 2][:, :, t, t * P : (t + 1) * P]
-                nc.vector.tensor_tensor(
+                nc.gpsimd.tensor_tensor(
                     out=block, in0=block, in1=keep[:].unsqueeze(1).to_broadcast([P, H, P]), op=ALU.mult
                 )
 
@@ -232,7 +233,7 @@ def tile_networklayer_pb_t_kernel(tc, q_pos, k_pos, x_grp, Wv_words, Wv_scales, 
                     words = x_rows[g][:, 2 * pair + j, :].bitcast(F32)
                     for u in range(2):
                         nc.tensor.transpose(x_ps[:, j, u, :], words[:, u : DM // 2 : 2], ident_f32[:])
-                nc.scalar.copy(
+                nc.vector.tensor_copy(
                     out=x_grouped[:].bitcast(F32)[:, 2 * pair : 2 * pair + 2, :, :],
                     in_=x_ps[:].rearrange("p j u c -> p j c u"),
                 )
@@ -286,11 +287,11 @@ def tile_networklayer_pb_t_kernel(tc, q_pos, k_pos, x_grp, Wv_words, Wv_scales, 
             if is_unit(tick - ACT_BEHIND):
                 activations(tick - ACT_BEHIND)
             if is_unit(tick - WEIGHTS_BEHIND):
-                if (tick - WEIGHTS_BEHIND) % H == 0:
-                    mask_diagonal((tick - WEIGHTS_BEHIND) // H)
                 regroup_w(tick - WEIGHTS_BEHIND)
             if is_unit(tick + NORMS_AHEAD):
                 norms(tick + NORMS_AHEAD)
+            if is_unit(tick - MASK_BEHIND) and (tick - MASK_BEHIND) % H == 0:
+                mask_diagonal((tick - MASK_BEHIND) // H)
             if is_unit(tick):
                 scores(tick)
             if is_unit(tick - WEIGHTS_BEHIND):

@@ -27,9 +27,10 @@ TRANSPOSE_AHEAD = 3
 NORMS_AHEAD = 2
 Q2_AHEAD = 1
 ACT_BEHIND = 3
-MASK_BEHIND = 7
-WEIGHTS_BEHIND = 8
-ATTEND_BEHIND = 9
+MASK_BEHIND = 4
+QUANT_BEHIND = 7
+ATTEND_BEHIND = 8
+MASKED_LN = 10000.0
 
 
 def tile_networklayer_pb_t_kernel(tc, q_pos, k_pos, x_grp, Wv_words, Wv_scales, bv, out):
@@ -45,7 +46,7 @@ def tile_networklayer_pb_t_kernel(tc, q_pos, k_pos, x_grp, Wv_words, Wv_scales, 
 
         q_rows, k_rows, x_rows = {}, {}, {}
         qk_t, q_sq, k2, k2_half, q2_half = {}, {}, {}, {}, {}
-        dist, grouped, w_codes, w_scl = {}, {}, {}, {}
+        dist, w_codes, w_scl = {}, {}, {}
         x_codes, x_scl, v_grouped, v_codes, v_scl = {}, {}, {}, {}, {}
 
         def load(g):
@@ -56,7 +57,15 @@ def tile_networklayer_pb_t_kernel(tc, q_pos, k_pos, x_grp, Wv_words, Wv_scales, 
             x_rows[g] = rows.tile([P, NT, DM], BF16, name="x_rows", tag="x_rows")
             nc.sync.dma_start(out=x_rows[g][:], in_=x_grp[g].rearrange("(t p) k -> p t k", p=P))
 
-        load(0)
+        q_rows[0] = rows.tile([P, H * NT, P], BF16, name="q_rows", tag="q_rows")
+        k_rows[0] = rows.tile([P, H * NT, P], BF16, name="k_rows", tag="k_rows")
+        x_rows[0] = rows.tile([P, NT, DM], BF16, name="x_rows", tag="x_rows")
+        for h in range(H):
+            tiles_of_head = slice(h * NT, (h + 1) * NT)
+            nc.sync.dma_start(out=q_rows[0][:, tiles_of_head, :], in_=q_pos[0, h].rearrange("(t p) d -> p t d", p=P))
+            nc.sync.dma_start(out=k_rows[0][:, tiles_of_head, :], in_=k_pos[0, h].rearrange("(t p) d -> p t d", p=P))
+            if h == 0:
+                nc.sync.dma_start(out=x_rows[0][:], in_=x_grp[0].rearrange("(t p) k -> p t k", p=P))
 
         wv_words = const.tile([P, 4 * DM], U8, name="wv_words", align_bytes=64)
         nc.sync.dma_start(
@@ -81,33 +90,25 @@ def tile_networklayer_pb_t_kernel(tc, q_pos, k_pos, x_grp, Wv_words, Wv_scales, 
         nc.vector.memset(neg_half[:], -0.5)
         table_warmer = const.tile([P, 1], F32, name="table_warmer")
         nc.scalar.activation(out=table_warmer[:], in_=neg_half[:, 0:1], func=ACT.Ln, scale=-2.0)
-        keep_f32 = const.tile([P, P], F32, name="keep_f32")
-        nc.gpsimd.memset(keep_f32[:], 1.0)
-        nc.gpsimd.affine_select(
-            out=keep_f32[:],
-            in_=keep_f32[:],
-            pattern=[[1, P]],
-            compare_op=ALU.is_ge,
-            fill=0.0,
-            base=0,
-            channel_multiplier=-1,
-        )
-        keep = const.tile([P, P], BF16, name="keep")
-        nc.vector.tensor_copy(out=keep[:], in_=keep_f32[:])
         squares_unused = const.tile([P, P], BF16, name="squares_unused")
-        w_planes = [const.tile([P, H, NT, B], BF16, name="w_planes%d" % i) for i in range(2)]
-        for planes in w_planes:
-            for t in range(1, NT):
-                nc.vector.memset(planes[:, :, t, : t * P], 0.0)
+        grouped = [const.tile([P, H, B, NT], BF16, name="grouped%d" % i, align_bytes=64) for i in range(2)]
+        for tile_ in grouped:
+            nc.gpsimd.memset(tile_[:].rearrange("p h b t -> p (h b t)").bitcast(F32), 0.0)
 
         def transpose_qk(u):
             g, h = divmod(u, H)
             qk_ps = ps_prep.tile([P, 2 * B], BF16, name="qk_ps", tag="prep")
             for t in range(NT):
-                nc.tensor.transpose(qk_ps[:, t * P : (t + 1) * P], q_rows[g][:, h * NT + t, :], ident_bf[:])
+                nc.tensor.matmul(
+                    qk_ps[:, t * P : (t + 1) * P], lhsT=q_rows[g][:, h * NT + t, :], rhs=ident_bf[:], start=True, stop=True
+                )
             for t in range(NT):
-                nc.tensor.transpose(
-                    qk_ps[:, B + t * P : B + (t + 1) * P], k_rows[g][:, h * NT + t, :], ident_bf[:]
+                nc.tensor.matmul(
+                    qk_ps[:, B + t * P : B + (t + 1) * P],
+                    lhsT=k_rows[g][:, h * NT + t, :],
+                    rhs=ident_bf[:],
+                    start=True,
+                    stop=True,
                 )
             qk_t[u] = work.tile([P, 2 * B], BF16, name="qk_t", tag="qk_t", bufs=5)
             nc.vector.tensor_copy(out=qk_t[u][:], in_=qk_ps[:])
@@ -141,7 +142,7 @@ def tile_networklayer_pb_t_kernel(tc, q_pos, k_pos, x_grp, Wv_words, Wv_scales, 
         def scores(u):
             g, h = divmod(u, H)
             if h == 0:
-                dist[g] = work.tile([P, H, LIVE], F32, name="dist", tag="dist")
+                dist[g] = work.tile([P, H, NT, B], F32, name="dist", tag="dist")
             for t in range(NT):
                 n = PLANE_COLS[t]
                 kq_ps = ps_score.tile([P, B], F32, name="kq_ps", tag="kq")
@@ -162,7 +163,7 @@ def tile_networklayer_pb_t_kernel(tc, q_pos, k_pos, x_grp, Wv_words, Wv_scales, 
                         stop=(i == NT - 1),
                     )
                 nc.vector.tensor_scalar(
-                    out=dist[g][:, h, PLANE_AT[t] : PLANE_AT[t] + n],
+                    out=dist[g][:, h, t, :n],
                     in0=kq_ps[:, :n],
                     scalar1=k2_half[u][:, t : t + 1],
                     scalar2=-0.5 * D2_FLOOR,
@@ -172,31 +173,33 @@ def tile_networklayer_pb_t_kernel(tc, q_pos, k_pos, x_grp, Wv_words, Wv_scales, 
 
         def activations(step):
             g, quarter = divmod(step, 4)
+            heads = slice(2 * (quarter % 2), 2 * (quarter % 2) + 2)
             if quarter < 2:
-                two_heads = dist[g][:, 2 * quarter : 2 * quarter + 2, :]
-                nc.scalar.activation(out=two_heads, in_=two_heads, func=ACT.Ln, scale=-2.0)
+                for t in range(NT):
+                    live = dist[g][:, heads, t, : PLANE_COLS[t]]
+                    nc.scalar.activation(out=live, in_=live, func=ACT.Ln, scale=-2.0)
             else:
-                for t in (0, 3) if quarter == 2 else (1, 2):
+                flat = dist[g][:, heads, :, :].rearrange("p h t b -> p h (t b)")
+                for i in range(NT):
+                    tiles = flat[:, :, i * P : i * P + (i + 1) * (B - P)].rearrange("p h (t s) -> p h t s", s=B - P)
                     nc.scalar.activation(
-                        out=w_planes[g % 2][:, :, t, t * P :],
-                        in_=dist[g][:, :, PLANE_AT[t] : PLANE_AT[t] + PLANE_COLS[t]],
+                        out=grouped[g % 2][:, heads, i * P : (i + 1) * P, : i + 1],
+                        in_=tiles[:, :, :, :P].rearrange("p h t j -> p h j t"),
                         func=ACT.Sigmoid,
                         scale=-0.5,
                     )
 
-        def mask_diagonal(g):
-            for t in range(NT):
-                block = w_planes[g % 2][:, :, t, t * P : (t + 1) * P]
-                nc.gpsimd.tensor_tensor(
-                    out=block, in0=block, in1=keep[:].unsqueeze(1).to_broadcast([P, H, P]), op=ALU.mult
-                )
-
-        def regroup_w(u):
+        def mask_diagonal(u):
             g, h = divmod(u, H)
-            grouped[u] = work.tile([P, B, NT], BF16, name="grouped", tag="grouped", bufs=2, align_bytes=64)
-            nc.vector.tensor_copy(
-                out=grouped[u][:].rearrange("p (c i) t -> p c t i", i=4),
-                in_=w_planes[g % 2][:, h, :, :].rearrange("p t (c i) -> p c t i", i=4),
+            block = dist[g][:, h, :, :P]
+            nc.gpsimd.affine_select(
+                out=block,
+                in_=block,
+                pattern=[[0, NT], [1, P]],
+                compare_op=ALU.is_ge,
+                fill=MASKED_LN,
+                base=0,
+                channel_multiplier=-1,
             )
 
         def quantise_w(u):
@@ -205,7 +208,7 @@ def tile_networklayer_pb_t_kernel(tc, q_pos, k_pos, x_grp, Wv_words, Wv_scales, 
             nc.vector.quantize_mx(
                 out=w_codes[u][:].bitcast(FP8X4),
                 scales=w_scl[u][:],
-                in_=grouped[u][:].rearrange("p b t -> p (b t)"),
+                in_=grouped[(u // H) % 2][:, u % H, :, :].rearrange("p b t -> p (b t)"),
             )
 
         def attend(u):
@@ -222,7 +225,10 @@ def tile_networklayer_pb_t_kernel(tc, q_pos, k_pos, x_grp, Wv_words, Wv_scales, 
                     stop=True,
                 )
             o_sb = work.tile([P, NT, P], F32, name="o_sb", tag="o_sb")
-            nc.scalar.copy(out=o_sb[:], in_=o_ps[:])
+            if u % 4 < 4:
+                nc.vector.tensor_copy(out=o_sb[:], in_=o_ps[:])
+            else:
+                nc.scalar.copy(out=o_sb[:], in_=o_ps[:])
             nc.sync.dma_start(out=out[g, :, h * P : (h + 1) * P].rearrange("(i p) n -> p i n", p=P), in_=o_sb[:])
 
         def transpose_x(g):
@@ -286,16 +292,16 @@ def tile_networklayer_pb_t_kernel(tc, q_pos, k_pos, x_grp, Wv_words, Wv_scales, 
         for tick in range(-TRANSPOSE_AHEAD, UNITS + ATTEND_BEHIND):
             if is_unit(tick - ACT_BEHIND):
                 activations(tick - ACT_BEHIND)
-            if is_unit(tick - WEIGHTS_BEHIND):
-                regroup_w(tick - WEIGHTS_BEHIND)
             if is_unit(tick + NORMS_AHEAD):
                 norms(tick + NORMS_AHEAD)
-            if is_unit(tick - MASK_BEHIND) and (tick - MASK_BEHIND) % H == 0:
-                mask_diagonal((tick - MASK_BEHIND) // H)
+            if is_unit(tick - MASK_BEHIND) and (tick - MASK_BEHIND) % H < 2:
+                first = (tick - MASK_BEHIND) // H * H + 2 * ((tick - MASK_BEHIND) % H)
+                mask_diagonal(first)
+                mask_diagonal(first + 1)
             if is_unit(tick):
                 scores(tick)
-            if is_unit(tick - WEIGHTS_BEHIND):
-                quantise_w(tick - WEIGHTS_BEHIND)
+            if is_unit(tick - QUANT_BEHIND):
+                quantise_w(tick - QUANT_BEHIND)
             if is_unit(tick + Q2_AHEAD):
                 half_norms(tick + Q2_AHEAD)
             if is_unit(tick):

@@ -27,9 +27,8 @@ TRANSPOSE_AHEAD = 3
 NORMS_AHEAD = 2
 Q2_AHEAD = 1
 ACT_BEHIND = 3
-MASK_BEHIND = 4
-QUANT_BEHIND = 7
-ATTEND_BEHIND = 8
+BATCHES = [[0, 1], [2, 3], [4, 5], [6, 7]]
+GROUPED_BUFS = 3
 MASKED_LN = 10000.0
 
 
@@ -91,9 +90,11 @@ def tile_networklayer_pb_t_kernel(tc, q_pos, k_pos, x_grp, Wv_words, Wv_scales, 
         table_warmer = const.tile([P, 1], F32, name="table_warmer")
         nc.scalar.activation(out=table_warmer[:], in_=neg_half[:, 0:1], func=ACT.Ln, scale=-2.0)
         squares_unused = const.tile([P, P], BF16, name="squares_unused")
-        grouped = [const.tile([P, H, B, NT], BF16, name="grouped%d" % i, align_bytes=64) for i in range(2)]
-        for tile_ in grouped:
-            nc.gpsimd.memset(tile_[:].rearrange("p h b t -> p (h b t)").bitcast(F32), 0.0)
+        grouped = [const.tile([P, H, B, NT], BF16, name="grouped%d" % i, align_bytes=64) for i in range(GROUPED_BUFS)]
+        def zero_grouped(i):
+            nc.gpsimd.memset(grouped[i][:].rearrange("p h b t -> p (h b t)").bitcast(F32), 0.0)
+
+        zero_grouped(0)
 
         def transpose_qk(u):
             g, h = divmod(u, H)
@@ -115,9 +116,12 @@ def tile_networklayer_pb_t_kernel(tc, q_pos, k_pos, x_grp, Wv_words, Wv_scales, 
 
         def norms(u):
             g, h = divmod(u, H)
-            q_sq[u] = work.tile([P, B], F32, name="q_sq", tag="q_sq")
+            q_sq[u] = work.tile([P, B], F32, name="q_sq", tag="q_sq", bufs=2)
             nc.gpsimd.tensor_tensor(out=q_sq[u][:], in0=qk_t[u][:, :B], in1=qk_t[u][:, :B], op=ALU.mult)
-            k2[u] = work.tile([P, NT], F32, name="k2", tag="k2", bufs=4)
+
+        def k_norms(u):
+            g, h = divmod(u, H)
+            k2[u] = work.tile([P, NT], F32, name="k2", tag="k2", bufs=5 + 3)
             for t in range(NT):
                 nc.scalar.activation(
                     out=squares_unused[:],
@@ -171,8 +175,7 @@ def tile_networklayer_pb_t_kernel(tc, q_pos, k_pos, x_grp, Wv_words, Wv_scales, 
                     op1=ALU.min,
                 )
 
-        def activations(step):
-            g, quarter = divmod(step, 4)
+        def activations(g, quarter):
             heads = slice(2 * (quarter % 2), 2 * (quarter % 2) + 2)
             if quarter < 2:
                 for t in range(NT):
@@ -183,7 +186,7 @@ def tile_networklayer_pb_t_kernel(tc, q_pos, k_pos, x_grp, Wv_words, Wv_scales, 
                 for i in range(NT):
                     tiles = flat[:, :, i * P : i * P + (i + 1) * (B - P)].rearrange("p h (t s) -> p h t s", s=B - P)
                     nc.scalar.activation(
-                        out=grouped[g % 2][:, heads, i * P : (i + 1) * P, : i + 1],
+                        out=grouped[g % GROUPED_BUFS][:, heads, i * P : (i + 1) * P, : i + 1],
                         in_=tiles[:, :, :, :P].rearrange("p h t j -> p h j t"),
                         func=ACT.Sigmoid,
                         scale=-0.5,
@@ -208,7 +211,7 @@ def tile_networklayer_pb_t_kernel(tc, q_pos, k_pos, x_grp, Wv_words, Wv_scales, 
             nc.vector.quantize_mx(
                 out=w_codes[u][:].bitcast(FP8X4),
                 scales=w_scl[u][:],
-                in_=grouped[(u // H) % 2][:, u % H, :, :].rearrange("p b t -> p (b t)"),
+                in_=grouped[(u // H) % GROUPED_BUFS][:, u % H, :, :].rearrange("p b t -> p (b t)"),
             )
 
         def attend(u):
@@ -277,8 +280,8 @@ def tile_networklayer_pb_t_kernel(tc, q_pos, k_pos, x_grp, Wv_words, Wv_scales, 
             )
 
         def quantise_v(g):
-            v_codes[g] = work.tile([P, DM], U32, name="v_codes", tag="v_codes", align_bytes=64)
-            v_scl[g] = work.tile([P, DM], U8, name="v_scl", tag="v_scl", align_bytes=64)
+            v_codes[g] = work.tile([P, DM], U32, name="v_codes", tag="v_codes", bufs=4, align_bytes=64)
+            v_scl[g] = work.tile([P, DM], U8, name="v_scl", tag="v_scl", bufs=4, align_bytes=64)
             nc.vector.quantize_mx(
                 out=v_codes[g][:].bitcast(FP8X4),
                 scales=v_scl[g][:],
@@ -288,28 +291,54 @@ def tile_networklayer_pb_t_kernel(tc, q_pos, k_pos, x_grp, Wv_words, Wv_scales, 
         def is_unit(u):
             return 0 <= u < UNITS
 
+        act_at, mask_at, weights_at, sigmoid_tick = {}, {}, {}, {}
+        at = 0
+        for batch in BATCHES:
+            for quarters in ((0, 1), (2, 3)):
+                for g in batch:
+                    for quarter in quarters:
+                        at = max(at + 1, H * g + ACT_BEHIND + quarter) if quarter < 2 else at + 1
+                        act_at[at] = (g, quarter)
+                        if quarter < 2:
+                            mask_at[at + 1] = H * g + 2 * quarter
+                        else:
+                            sigmoid_tick[(g, quarter - 2)] = at
+        at = 0
+        for u in range(UNITS):
+            at = max(at + 1, sigmoid_tick[(u // H, u % H // 2)] + 2)
+            weights_at[at] = u
+        last_tick = at + 1
+        done_at = dict((u, tick) for tick, u in weights_at.items())
+        for g in range(S):
+            assert g < GROUPED_BUFS or done_at[H * (g - GROUPED_BUFS) + H - 1] < sigmoid_tick[(g, 0)]
+            assert g < 3 or sigmoid_tick[(g - 3, 1)] < H * g
+            assert g < 4 or done_at[H * (g - 4) + H - 1] + 1 < H * g + H
+
         x_waiting = {}
-        for tick in range(-TRANSPOSE_AHEAD, UNITS + ATTEND_BEHIND):
-            if is_unit(tick - ACT_BEHIND):
-                activations(tick - ACT_BEHIND)
+        for tick in range(-max(TRANSPOSE_AHEAD, 5), last_tick + 1):
+            if tick in act_at:
+                activations(act_at[tick][0], act_at[tick][1])
             if is_unit(tick + NORMS_AHEAD):
                 norms(tick + NORMS_AHEAD)
-            if is_unit(tick - MASK_BEHIND) and (tick - MASK_BEHIND) % H < 2:
-                first = (tick - MASK_BEHIND) // H * H + 2 * ((tick - MASK_BEHIND) % H)
-                mask_diagonal(first)
-                mask_diagonal(first + 1)
+            if is_unit(tick + 5):
+                k_norms(tick + 5)
+            if tick in (1, 3) and (tick + 1) // 2 < GROUPED_BUFS:
+                zero_grouped((tick + 1) // 2)
+            if tick in mask_at:
+                mask_diagonal(mask_at[tick])
+                mask_diagonal(mask_at[tick] + 1)
             if is_unit(tick):
                 scores(tick)
-            if is_unit(tick - QUANT_BEHIND):
-                quantise_w(tick - QUANT_BEHIND)
+            if tick in weights_at:
+                quantise_w(weights_at[tick])
             if is_unit(tick + Q2_AHEAD):
                 half_norms(tick + Q2_AHEAD)
             if is_unit(tick):
                 project_values(tick)
             if is_unit(tick - H) and tick % H == 0:
                 quantise_v(tick // H - 1)
-            if is_unit(tick - ATTEND_BEHIND):
-                attend(tick - ATTEND_BEHIND)
+            if tick - 1 in weights_at:
+                attend(weights_at[tick - 1])
             if is_unit(tick + TRANSPOSE_AHEAD):
                 transpose_qk(tick + TRANSPOSE_AHEAD)
             if is_unit(tick + 2) and (tick + 2) % H == 0:

@@ -44,7 +44,7 @@ def tile_networklayer_pb_t_kernel(tc, q_pos, k_pos, x_grp, Wv_words, Wv_scales, 
         ctx.enter_context(tc.manual_schedule())
 
         q_rows, k_rows, x_rows = {}, {}, {}
-        qk_t, q_sq, k2, k2_half, q2_half = {}, {}, {}, {}, {}
+        qk_t, q_sq, q_sq_low, k2, q2_half = {}, {}, {}, {}, {}
         dist, w_codes, w_scl = {}, {}, {}
         x_codes, x_scl, v_grouped, v_codes, v_scl = {}, {}, {}, {}, {}
 
@@ -83,6 +83,10 @@ def tile_networklayer_pb_t_kernel(tc, q_pos, k_pos, x_grp, Wv_words, Wv_scales, 
 
         ident_bf = const.tile([P, P], BF16, name="ident_bf")
         make_identity(nc, ident_bf[:])
+        twice_ident = const.tile([P, P], BF16, name="twice_ident")
+        nc.vector.tensor_scalar(out=twice_ident[:], in0=ident_bf[:], scalar1=2.0, scalar2=0.0, op0=ALU.mult, op1=ALU.add)
+        minus_one = const.tile([P, 2], BF16, name="minus_one")
+        nc.vector.memset(minus_one[:], -1.0)
         ident_f32 = const.tile([P, P], F32, name="ident_f32")
         make_identity(nc, ident_f32[:])
         neg_half = const.tile([P, P], F32, name="neg_half")
@@ -107,7 +111,7 @@ def tile_networklayer_pb_t_kernel(tc, q_pos, k_pos, x_grp, Wv_words, Wv_scales, 
                 nc.tensor.matmul(
                     qk_ps[:, B + t * P : B + (t + 1) * P],
                     lhsT=k_rows[g][:, h * NT + t, :],
-                    rhs=ident_bf[:],
+                    rhs=twice_ident[:],
                     start=True,
                     stop=True,
                 )
@@ -118,6 +122,10 @@ def tile_networklayer_pb_t_kernel(tc, q_pos, k_pos, x_grp, Wv_words, Wv_scales, 
             g, h = divmod(u, H)
             q_sq[u] = work.tile([P, B], F32, name="q_sq", tag="q_sq", bufs=2)
             nc.gpsimd.tensor_tensor(out=q_sq[u][:], in0=qk_t[u][:, :B], in1=qk_t[u][:, :B], op=ALU.mult)
+            q_sq_low[u] = work.tile([P, B], BF16, name="q_sq_low", tag="q_sq_low", bufs=2)
+            nc.gpsimd.tensor_tensor(
+                out=q_sq_low[u][:], in0=q_sq[u][:], in1=q_sq[u][:].bitcast(BF16)[:, 1 : 2 * B : 2], op=ALU.subtract
+            )
 
         def k_norms(u):
             g, h = divmod(u, H)
@@ -132,16 +140,20 @@ def tile_networklayer_pb_t_kernel(tc, q_pos, k_pos, x_grp, Wv_words, Wv_scales, 
 
         def half_norms(u):
             q2_ps = ps_prep.tile([P, NT, 2], F32, name="q2_ps", tag="prep")
+            upper = q_sq[u][:].bitcast(BF16)
             for i in range(NT):
                 nc.tensor.matmul(
-                    q2_ps[:, i, :], lhsT=q_sq[u][:, i * P : (i + 1) * P], rhs=neg_half[:, 0:2], start=True, stop=True
+                    q2_ps[:, i, :],
+                    lhsT=upper[:, 2 * i * P + 1 : 2 * (i + 1) * P : 2],
+                    rhs=minus_one[:, 0:2],
+                    start=True,
+                    stop=False,
+                )
+                nc.tensor.matmul(
+                    q2_ps[:, i, :], lhsT=q_sq_low[u][:, i * P : (i + 1) * P], rhs=minus_one[:, 0:2], start=False, stop=True
                 )
             q2_half[u] = work.tile([P, NT, 2], F32, name="q2_half", tag="q2_half", bufs=4)
             nc.vector.tensor_copy(out=q2_half[u][:], in_=q2_ps[:])
-            k2_half[u] = work.tile([P, NT], F32, name="k2_half", tag="k2_half", bufs=4)
-            nc.gpsimd.tensor_scalar(
-                out=k2_half[u][:], in0=k2[u][:], scalar1=-0.5, scalar2=0.0, op0=ALU.mult, op1=ALU.add
-            )
 
         def scores(u):
             g, h = divmod(u, H)
@@ -169,9 +181,9 @@ def tile_networklayer_pb_t_kernel(tc, q_pos, k_pos, x_grp, Wv_words, Wv_scales, 
                 nc.vector.tensor_scalar(
                     out=dist[g][:, h, t, :n],
                     in0=kq_ps[:, :n],
-                    scalar1=k2_half[u][:, t : t + 1],
-                    scalar2=-0.5 * D2_FLOOR,
-                    op0=ALU.add,
+                    scalar1=k2[u][:, t : t + 1],
+                    scalar2=-D2_FLOOR,
+                    op0=ALU.subtract,
                     op1=ALU.min,
                 )
 
@@ -180,7 +192,7 @@ def tile_networklayer_pb_t_kernel(tc, q_pos, k_pos, x_grp, Wv_words, Wv_scales, 
             if quarter < 2:
                 for t in range(NT):
                     live = dist[g][:, heads, t, : PLANE_COLS[t]]
-                    nc.scalar.activation(out=live, in_=live, func=ACT.Ln, scale=-2.0)
+                    nc.scalar.activation(out=live, in_=live, func=ACT.Ln, scale=-1.0)
             else:
                 flat = dist[g][:, heads, :, :].rearrange("p h t b -> p h (t b)")
                 for i in range(NT):

@@ -48,16 +48,18 @@ def tile_networklayer_pb_t_kernel(tc, q_pos, k_pos, x_grp, Wv_words, Wv_scales, 
         dist, w_codes, w_scl = {}, {}, {}
         x_codes, x_scl, v_grouped, v_codes, v_scl = {}, {}, {}, {}, {}
 
+        def load_k(g):
+            k_rows[g] = rows.tile([P, H * NT, P], BF16, name="k_rows", tag="k_rows", bufs=3)
+            nc.sync.dma_start(out=k_rows[g][:], in_=k_pos[g].rearrange("h (t p) d -> p (h t) d", p=P))
+
         def load(g):
             q_rows[g] = rows.tile([P, H * NT, P], BF16, name="q_rows", tag="q_rows")
             nc.sync.dma_start(out=q_rows[g][:], in_=q_pos[g].rearrange("h (t p) d -> p (h t) d", p=P))
-            k_rows[g] = rows.tile([P, H * NT, P], BF16, name="k_rows", tag="k_rows")
-            nc.sync.dma_start(out=k_rows[g][:], in_=k_pos[g].rearrange("h (t p) d -> p (h t) d", p=P))
             x_rows[g] = rows.tile([P, NT, DM], BF16, name="x_rows", tag="x_rows")
             nc.sync.dma_start(out=x_rows[g][:], in_=x_grp[g].rearrange("(t p) k -> p t k", p=P))
 
         q_rows[0] = rows.tile([P, H * NT, P], BF16, name="q_rows", tag="q_rows")
-        k_rows[0] = rows.tile([P, H * NT, P], BF16, name="k_rows", tag="k_rows")
+        k_rows[0] = rows.tile([P, H * NT, P], BF16, name="k_rows", tag="k_rows", bufs=3)
         x_rows[0] = rows.tile([P, NT, DM], BF16, name="x_rows", tag="x_rows")
         for h in range(H):
             tiles_of_head = slice(h * NT, (h + 1) * NT)
@@ -79,7 +81,9 @@ def tile_networklayer_pb_t_kernel(tc, q_pos, k_pos, x_grp, Wv_words, Wv_scales, 
             )
         bias_bc = const.tile([P, DM], BF16, name="bias_bc")
         nc.sync.dma_start(out=bias_bc[:], in_=bv.partition_broadcast(P))
+        load_k(1)
         load(1)
+        load_k(2)
 
         ident_bf = const.tile([P, P], BF16, name="ident_bf")
         make_identity(nc, ident_bf[:])
@@ -89,12 +93,14 @@ def tile_networklayer_pb_t_kernel(tc, q_pos, k_pos, x_grp, Wv_words, Wv_scales, 
         nc.vector.memset(minus_one[:], -1.0)
         ident_f32 = const.tile([P, P], F32, name="ident_f32")
         make_identity(nc, ident_f32[:])
-        neg_half = const.tile([P, P], F32, name="neg_half")
+        neg_half = const.tile([P, 2], F32, name="neg_half")
         nc.vector.memset(neg_half[:], -0.5)
         table_warmer = const.tile([P, 1], F32, name="table_warmer")
         nc.scalar.activation(out=table_warmer[:], in_=neg_half[:, 0:1], func=ACT.Ln, scale=-2.0)
         squares_unused = const.tile([P, P], BF16, name="squares_unused")
         grouped = [const.tile([P, H, B, NT], BF16, name="grouped%d" % i, align_bytes=64) for i in range(GROUPED_BUFS)]
+        first_tile = [const.tile([P, H, P], BF16, name="first_tile%d" % i) for i in range(GROUPED_BUFS)]
+
         def zero_grouped(i):
             nc.gpsimd.memset(grouped[i][:].rearrange("p h b t -> p (h b t)").bitcast(F32), 0.0)
 
@@ -115,7 +121,7 @@ def tile_networklayer_pb_t_kernel(tc, q_pos, k_pos, x_grp, Wv_words, Wv_scales, 
                     start=True,
                     stop=True,
                 )
-            qk_t[u] = work.tile([P, 2 * B], BF16, name="qk_t", tag="qk_t", bufs=5)
+            qk_t[u] = work.tile([P, 2 * B], BF16, name="qk_t", tag="qk_t", bufs=4)
             nc.vector.tensor_copy(out=qk_t[u][:], in_=qk_ps[:])
 
         def norms(u):
@@ -129,7 +135,7 @@ def tile_networklayer_pb_t_kernel(tc, q_pos, k_pos, x_grp, Wv_words, Wv_scales, 
 
         def k_norms(u):
             g, h = divmod(u, H)
-            k2[u] = work.tile([P, NT], F32, name="k2", tag="k2", bufs=5 + 3)
+            k2[u] = work.tile([P, NT], F32, name="k2", tag="k2", bufs=9 + 3)
             for t in range(NT):
                 nc.scalar.activation(
                     out=squares_unused[:],
@@ -188,14 +194,35 @@ def tile_networklayer_pb_t_kernel(tc, q_pos, k_pos, x_grp, Wv_words, Wv_scales, 
                 )
 
         def activations(g, quarter):
-            heads = slice(2 * (quarter % 2), 2 * (quarter % 2) + 2)
             if quarter < 2:
+                if 0:
+                    if quarter == 0:
+                        return
+                    heads = slice(0, H)
+                else:
+                    heads = slice(2 * quarter, 2 * quarter + 2)
                 for t in range(NT):
                     live = dist[g][:, heads, t, : PLANE_COLS[t]]
                     nc.scalar.activation(out=live, in_=live, func=ACT.Ln, scale=-1.0)
+                return
+            if 0 and g < S - 1:
+                if quarter == 3:
+                    return
+                parts = [slice(0, H)]
+            elif 1 and g == S - 1 and quarter == 3:
+                parts = [slice(2, 3), slice(3, 4)]
             else:
+                parts = [slice(2 * quarter - 4, 2 * quarter - 2)]
+            for heads in parts:
                 flat = dist[g][:, heads, :, :].rearrange("p h t b -> p h (t b)")
-                for i in range(NT):
+                if 1:
+                    nc.scalar.activation(
+                        out=first_tile[g % GROUPED_BUFS][:, heads, :],
+                        in_=dist[g][:, heads, 0, :P],
+                        func=ACT.Sigmoid,
+                        scale=-0.5,
+                    )
+                for i in range(1 if 1 else 0, NT):
                     tiles = flat[:, :, i * P : i * P + (i + 1) * (B - P)].rearrange("p h (t s) -> p h t s", s=B - P)
                     nc.scalar.activation(
                         out=grouped[g % GROUPED_BUFS][:, heads, i * P : (i + 1) * P, : i + 1],
@@ -206,20 +233,42 @@ def tile_networklayer_pb_t_kernel(tc, q_pos, k_pos, x_grp, Wv_words, Wv_scales, 
 
         def mask_diagonal(u):
             g, h = divmod(u, H)
-            block = dist[g][:, h, :, :P]
+            first = 1 if 1 else 0
+            block = dist[g][:, h, first:, :P]
             nc.gpsimd.affine_select(
                 out=block,
                 in_=block,
-                pattern=[[0, NT], [1, P]],
+                pattern=[[0, NT - first], [1, P]],
                 compare_op=ALU.is_ge,
                 fill=MASKED_LN,
                 base=0,
                 channel_multiplier=-1,
             )
 
+        def place_first_tile(g, pair):
+            heads = slice(2 * pair, 2 * pair + 2)
+            block = first_tile[g % GROUPED_BUFS][:, heads, :]
+            nc.gpsimd.affine_select(
+                out=block,
+                in_=block,
+                pattern=[[0, 2], [1, P]],
+                compare_op=ALU.is_ge,
+                fill=0.0,
+                base=0,
+                channel_multiplier=-1,
+            )
+            (nc.vector if 0 else nc.gpsimd).tensor_scalar(
+                out=grouped[g % GROUPED_BUFS][:, heads, :P, 0],
+                in0=block,
+                scalar1=1.0,
+                scalar2=0.0,
+                op0=ALU.mult,
+                op1=ALU.add,
+            )
+
         def quantise_w(u):
-            w_codes[u] = work.tile([P, B], U32, name="w_codes", tag="w_codes", align_bytes=64)
-            w_scl[u] = work.tile([P, B], U8, name="w_scl", tag="w_scl", align_bytes=64)
+            w_codes[u] = work.tile([P, B], U32, name="w_codes", tag="w_codes", bufs=2, align_bytes=64)
+            w_scl[u] = work.tile([P, B], U8, name="w_scl", tag="w_scl", bufs=2, align_bytes=64)
             nc.vector.quantize_mx(
                 out=w_codes[u][:].bitcast(FP8X4),
                 scales=w_scl[u][:],
@@ -239,7 +288,7 @@ def tile_networklayer_pb_t_kernel(tc, q_pos, k_pos, x_grp, Wv_words, Wv_scales, 
                     start=True,
                     stop=True,
                 )
-            o_sb = work.tile([P, NT, P], F32, name="o_sb", tag="o_sb")
+            o_sb = work.tile([P, NT, P], F32, name="o_sb", tag="o_sb", bufs=3)
             if u % 4 < 4:
                 nc.vector.tensor_copy(out=o_sb[:], in_=o_ps[:])
             else:
@@ -312,7 +361,9 @@ def tile_networklayer_pb_t_kernel(tc, q_pos, k_pos, x_grp, Wv_words, Wv_scales, 
                         at = max(at + 1, H * g + ACT_BEHIND + quarter) if quarter < 2 else at + 1
                         act_at[at] = (g, quarter)
                         if quarter < 2:
-                            mask_at[at + 1] = H * g + 2 * quarter
+                            mask_at[at + 1 + (0 and quarter == 0)] = H * g + 2 * quarter
+                            if 0 and quarter == 1:
+                                mask_at[at + 2] = H * g + 2
                         else:
                             sigmoid_tick[(g, quarter - 2)] = at
         at = 0
@@ -327,18 +378,20 @@ def tile_networklayer_pb_t_kernel(tc, q_pos, k_pos, x_grp, Wv_words, Wv_scales, 
             assert g < 4 or done_at[H * (g - 4) + H - 1] + 1 < H * g + H
 
         x_waiting = {}
-        for tick in range(-max(TRANSPOSE_AHEAD, 5), last_tick + 1):
+        for tick in range(-max(TRANSPOSE_AHEAD, 9), last_tick + 1):
             if tick in act_at:
                 activations(act_at[tick][0], act_at[tick][1])
             if is_unit(tick + NORMS_AHEAD):
                 norms(tick + NORMS_AHEAD)
-            if is_unit(tick + 5):
-                k_norms(tick + 5)
+            if is_unit(tick + 9):
+                k_norms(tick + 9)
             if tick in (1, 3) and (tick + 1) // 2 < GROUPED_BUFS:
                 zero_grouped((tick + 1) // 2)
             if tick in mask_at:
                 mask_diagonal(mask_at[tick])
                 mask_diagonal(mask_at[tick] + 1)
+            if 1 and tick - 1 in act_at and act_at[tick - 1][1] >= 2:
+                place_first_tile(act_at[tick - 1][0], act_at[tick - 1][1] - 2)
             if is_unit(tick):
                 scores(tick)
             if tick in weights_at:
@@ -360,3 +413,5 @@ def tile_networklayer_pb_t_kernel(tc, q_pos, k_pos, x_grp, Wv_words, Wv_scales, 
             if is_unit(tick + NORMS_AHEAD) and (tick + NORMS_AHEAD) % H == H - 1:
                 if (tick + NORMS_AHEAD) // H + 2 < S:
                     load((tick + NORMS_AHEAD) // H + 2)
+                if (tick + NORMS_AHEAD) // H + 3 < S:
+                    load_k((tick + NORMS_AHEAD) // H + 3)

@@ -93,6 +93,8 @@ def tile_networklayer_pb_t_kernel(tc, q_pos, k_pos, x_grp, Wv_words, Wv_scales, 
         nc.vector.memset(minus_one[:], -1.0)
         ident_f32 = const.tile([P, P], F32, name="ident_f32")
         make_identity(nc, ident_f32[:])
+        minus_one_f32 = const.tile([P, 2], F32, name="minus_one_f32")
+        nc.vector.memset(minus_one_f32[:], -1.0)
         neg_half = const.tile([P, 2], F32, name="neg_half")
         nc.vector.memset(neg_half[:], -0.5)
         table_warmer = const.tile([P, 1], F32, name="table_warmer")
@@ -124,10 +126,15 @@ def tile_networklayer_pb_t_kernel(tc, q_pos, k_pos, x_grp, Wv_words, Wv_scales, 
             qk_t[u] = work.tile([P, 2 * B], BF16, name="qk_t", tag="qk_t", bufs=4)
             nc.vector.tensor_copy(out=qk_t[u][:], in_=qk_ps[:])
 
+        def halves(u):
+            return u % 2 < 1
+
         def norms(u):
             g, h = divmod(u, H)
             q_sq[u] = work.tile([P, B], F32, name="q_sq", tag="q_sq", bufs=2)
             nc.gpsimd.tensor_tensor(out=q_sq[u][:], in0=qk_t[u][:, :B], in1=qk_t[u][:, :B], op=ALU.mult)
+            if not halves(u):
+                return
             q_sq_low[u] = work.tile([P, B], BF16, name="q_sq_low", tag="q_sq_low", bufs=2)
             nc.gpsimd.tensor_tensor(
                 out=q_sq_low[u][:], in0=q_sq[u][:], in1=q_sq[u][:].bitcast(BF16)[:, 1 : 2 * B : 2], op=ALU.subtract
@@ -148,6 +155,11 @@ def tile_networklayer_pb_t_kernel(tc, q_pos, k_pos, x_grp, Wv_words, Wv_scales, 
             q2_ps = ps_prep.tile([P, NT, 2], F32, name="q2_ps", tag="prep")
             upper = q_sq[u][:].bitcast(BF16)
             for i in range(NT):
+                if not halves(u):
+                    nc.tensor.matmul(
+                        q2_ps[:, i, :], lhsT=q_sq[u][:, i * P : (i + 1) * P], rhs=minus_one_f32[:, 0:2], start=True, stop=True
+                    )
+                    continue
                 nc.tensor.matmul(
                     q2_ps[:, i, :],
                     lhsT=upper[:, 2 * i * P + 1 : 2 * (i + 1) * P : 2],
@@ -193,6 +205,11 @@ def tile_networklayer_pb_t_kernel(tc, q_pos, k_pos, x_grp, Wv_words, Wv_scales, 
                     op1=ALU.min,
                 )
 
+        def sigmoid_parts(g, quarter):
+            if g == S - 1 and quarter == 3:
+                return [slice(2, 3), slice(3, 4)]
+            return [slice(2 * quarter - 4, 2 * quarter - 2)]
+
         def activations(g, quarter):
             if quarter < 2:
                 if 0:
@@ -205,15 +222,7 @@ def tile_networklayer_pb_t_kernel(tc, q_pos, k_pos, x_grp, Wv_words, Wv_scales, 
                     live = dist[g][:, heads, t, : PLANE_COLS[t]]
                     nc.scalar.activation(out=live, in_=live, func=ACT.Ln, scale=-1.0)
                 return
-            if 0 and g < S - 1:
-                if quarter == 3:
-                    return
-                parts = [slice(0, H)]
-            elif 1 and g == S - 1 and quarter == 3:
-                parts = [slice(2, 3), slice(3, 4)]
-            else:
-                parts = [slice(2 * quarter - 4, 2 * quarter - 2)]
-            for heads in parts:
+            for heads in sigmoid_parts(g, quarter):
                 flat = dist[g][:, heads, :, :].rearrange("p h t b -> p h (t b)")
                 if 1:
                     nc.scalar.activation(
@@ -245,13 +254,12 @@ def tile_networklayer_pb_t_kernel(tc, q_pos, k_pos, x_grp, Wv_words, Wv_scales, 
                 channel_multiplier=-1,
             )
 
-        def place_first_tile(g, pair):
-            heads = slice(2 * pair, 2 * pair + 2)
+        def place_first_tile(g, heads):
             block = first_tile[g % GROUPED_BUFS][:, heads, :]
             nc.gpsimd.affine_select(
                 out=block,
                 in_=block,
-                pattern=[[0, 2], [1, P]],
+                pattern=[[0, heads.stop - heads.start], [1, P]],
                 compare_op=ALU.is_ge,
                 fill=0.0,
                 base=0,
@@ -391,7 +399,8 @@ def tile_networklayer_pb_t_kernel(tc, q_pos, k_pos, x_grp, Wv_words, Wv_scales, 
                 mask_diagonal(mask_at[tick])
                 mask_diagonal(mask_at[tick] + 1)
             if 1 and tick - 1 in act_at and act_at[tick - 1][1] >= 2:
-                place_first_tile(act_at[tick - 1][0], act_at[tick - 1][1] - 2)
+                for heads in sigmoid_parts(act_at[tick - 1][0], act_at[tick - 1][1]):
+                    place_first_tile(act_at[tick - 1][0], heads)
             if is_unit(tick):
                 scores(tick)
             if tick in weights_at:

from contextlib import ExitStack

import concourse.mybir as mybir
from concourse.masks import make_identity

S, H, B, DM = 8, 4, 512, 512
P = 128
NT = B // P
UNITS = S * H
FLOPS = 3 * 2 * S * B * B * DM

BF16 = mybir.dt.bfloat16
F32 = mybir.dt.float32
I32 = mybir.dt.int32
U8 = mybir.dt.uint8
U32 = mybir.dt.uint32
FP8X4 = mybir.dt.float8_e4m3fn_x4
ALU = mybir.AluOpType
ACT = mybir.ActivationFunctionType

PLANE_COLS = [B - t * P for t in range(NT)]
PLANE_AT = [sum(PLANE_COLS[:t]) for t in range(NT)]
LIVE = sum(PLANE_COLS)
D2_FLOOR = 1e-12

TRANSPOSE_AHEAD = 3
NORMS_AHEAD = 2
Q2_AHEAD = 1
ACT_BEHIND = 3
BATCHES = [[0, 1], [2, 3], [4, 5], [6, 7]]
GROUPED_BUFS = 3
MASKED_LN = 10000.0


def tile_networklayer_pb_t_kernel(tc, q_pos, k_pos, x_grp, Wv_words, Wv_scales, bv, out):
    nc = tc.nc
    with ExitStack() as ctx:
        const = ctx.enter_context(tc.tile_pool(name="const", bufs=1))
        rows = ctx.enter_context(tc.tile_pool(name="rows", bufs=2))
        work = ctx.enter_context(tc.tile_pool(name="work", bufs=3))
        ps_score = ctx.enter_context(tc.psum_pool(name="ps_score", bufs=NT))
        ps_prep = ctx.enter_context(tc.psum_pool(name="ps_prep", bufs=3))
        ps_out = ctx.enter_context(tc.psum_pool(name="ps_out", bufs=1))
        ctx.enter_context(tc.manual_schedule())

        q_rows, k_rows, x_rows = {}, {}, {}
        qk_t, q_sq, q_sq_low, k2, q2_half = {}, {}, {}, {}, {}
        dist, w_codes, w_scl = {}, {}, {}
        x_codes, x_scl, v_grouped, v_codes, v_scl = {}, {}, {}, {}, {}

        def load_k(g):
            k_rows[g] = rows.tile([P, H * NT, P], BF16, name="k_rows", tag="k_rows", bufs=3)
            nc.sync.dma_start(out=k_rows[g][:], in_=k_pos[g].rearrange("h (t p) d -> p (h t) d", p=P))

        def load(g):
            q_rows[g] = rows.tile([P, H * NT, P], BF16, name="q_rows", tag="q_rows")
            nc.sync.dma_start(out=q_rows[g][:], in_=q_pos[g].rearrange("h (t p) d -> p (h t) d", p=P))
            x_rows[g] = rows.tile([P, NT, DM], BF16, name="x_rows", tag="x_rows")
            nc.sync.dma_start(out=x_rows[g][:], in_=x_grp[g].rearrange("(t p) k -> p t k", p=P))

        q_rows[0] = rows.tile([P, H * NT, P], BF16, name="q_rows", tag="q_rows")
        k_rows[0] = rows.tile([P, H * NT, P], BF16, name="k_rows", tag="k_rows", bufs=3)
        x_rows[0] = rows.tile([P, NT, DM], BF16, name="x_rows", tag="x_rows")
        for h in range(H):
            tiles_of_head = slice(h * NT, (h + 1) * NT)
            nc.sync.dma_start(out=q_rows[0][:, tiles_of_head, :], in_=q_pos[0, h].rearrange("(t p) d -> p t d", p=P))
            nc.sync.dma_start(out=k_rows[0][:, tiles_of_head, :], in_=k_pos[0, h].rearrange("(t p) d -> p t d", p=P))
            if h == 0:
                nc.sync.dma_start(out=x_rows[0][:], in_=x_grp[0].rearrange("(t p) k -> p t k", p=P))

        wv_words = const.tile([P, 4 * DM], U8, name="wv_words", align_bytes=64)
        nc.sync.dma_start(
            out=wv_words[:].bitcast(I32), in_=Wv_words[0].rearrange("p n t -> p (n t)").bitcast(I32)
        )
        wv_scl = const.tile([P, DM], U8, name="wv_scl", align_bytes=64)
        nc.vector.memset(wv_scl[:].bitcast(I32), 0)
        for quad in range(4):
            nc.sync.dma_start(
                out=wv_scl[32 * quad : 32 * quad + 4, :].bitcast(I32),
                in_=Wv_scales[0, 4 * quad : 4 * quad + 4, :].bitcast(I32),
            )
        bias_bc = const.tile([P, DM], BF16, name="bias_bc")
        nc.sync.dma_start(out=bias_bc[:], in_=bv.partition_broadcast(P))
        load_k(1)
        load(1)
        load_k(2)

        ident_bf = const.tile([P, P], BF16, name="ident_bf")
        make_identity(nc, ident_bf[:])
        twice_ident = const.tile([P, P], BF16, name="twice_ident")
        nc.vector.tensor_scalar(out=twice_ident[:], in0=ident_bf[:], scalar1=2.0, scalar2=0.0, op0=ALU.mult, op1=ALU.add)
        minus_one = const.tile([P, 2], BF16, name="minus_one")
        nc.vector.memset(minus_one[:], -1.0)
        ident_f32 = const.tile([P, P], F32, name="ident_f32")
        make_identity(nc, ident_f32[:])
        minus_one_f32 = const.tile([P, 2], F32, name="minus_one_f32")
        nc.vector.memset(minus_one_f32[:], -1.0)
        neg_half = const.tile([P, 2], F32, name="neg_half")
        nc.vector.memset(neg_half[:], -0.5)
        table_warmer = const.tile([P, 1], F32, name="table_warmer")
        nc.scalar.activation(out=table_warmer[:], in_=neg_half[:, 0:1], func=ACT.Ln, scale=-2.0)
        squares_unused = const.tile([P, P], BF16, name="squares_unused")
        grouped = [const.tile([P, H, B, NT], BF16, name="grouped%d" % i, align_bytes=64) for i in range(GROUPED_BUFS)]
        first_tile = [const.tile([P, H, P], BF16, name="first_tile%d" % i) for i in range(GROUPED_BUFS)]

        def zero_grouped(i):
            nc.gpsimd.memset(grouped[i][:].rearrange("p h b t -> p (h b t)").bitcast(F32), 0.0)

        zero_grouped(0)

        def transpose_qk(u):
            g, h = divmod(u, H)
            qk_ps = ps_prep.tile([P, 2 * B], BF16, name="qk_ps", tag="prep")
            for t in range(NT):
                nc.tensor.matmul(
                    qk_ps[:, t * P : (t + 1) * P], lhsT=q_rows[g][:, h * NT + t, :], rhs=ident_bf[:], start=True, stop=True
                )
            for t in range(NT):
                nc.tensor.matmul(
                    qk_ps[:, B + t * P : B + (t + 1) * P],
                    lhsT=k_rows[g][:, h * NT + t, :],
                    rhs=twice_ident[:],
                    start=True,
                    stop=True,
                )
            qk_t[u] = work.tile([P, 2 * B], BF16, name="qk_t", tag="qk_t", bufs=4)
            nc.vector.tensor_copy(out=qk_t[u][:], in_=qk_ps[:])

        def halves(u):
            return u % 2 < 1

        def norms(u):
            g, h = divmod(u, H)
            q_sq[u] = work.tile([P, B], F32, name="q_sq", tag="q_sq", bufs=2)
            nc.gpsimd.tensor_tensor(out=q_sq[u][:], in0=qk_t[u][:, :B], in1=qk_t[u][:, :B], op=ALU.mult)
            if not halves(u):
                return
            q_sq_low[u] = work.tile([P, B], BF16, name="q_sq_low", tag="q_sq_low", bufs=2)
            nc.gpsimd.tensor_tensor(
                out=q_sq_low[u][:], in0=q_sq[u][:], in1=q_sq[u][:].bitcast(BF16)[:, 1 : 2 * B : 2], op=ALU.subtract
            )

        def k_norms(u):
            g, h = divmod(u, H)
            k2[u] = work.tile([P, NT], F32, name="k2", tag="k2", bufs=9 + 3)
            for t in range(NT):
                nc.scalar.activation(
                    out=squares_unused[:],
                    in_=k_rows[g][:, h * NT + t, :],
                    func=ACT.Square,
                    accum_out=k2[u][:, t : t + 1],
                )

        def half_norms(u):
            q2_ps = ps_prep.tile([P, NT, 2], F32, name="q2_ps", tag="prep")
            upper = q_sq[u][:].bitcast(BF16)
            for i in range(NT):
                if not halves(u):
                    nc.tensor.matmul(
                        q2_ps[:, i, :], lhsT=q_sq[u][:, i * P : (i + 1) * P], rhs=minus_one_f32[:, 0:2], start=True, stop=True
                    )
                    continue
                nc.tensor.matmul(
                    q2_ps[:, i, :],
                    lhsT=upper[:, 2 * i * P + 1 : 2 * (i + 1) * P : 2],
                    rhs=minus_one[:, 0:2],
                    start=True,
                    stop=False,
                )
                nc.tensor.matmul(
                    q2_ps[:, i, :], lhsT=q_sq_low[u][:, i * P : (i + 1) * P], rhs=minus_one[:, 0:2], start=False, stop=True
                )
            q2_half[u] = work.tile([P, NT, 2], F32, name="q2_half", tag="q2_half", bufs=4)
            nc.vector.tensor_copy(out=q2_half[u][:], in_=q2_ps[:])

        def scores(u):
            g, h = divmod(u, H)
            if h == 0:
                dist[g] = work.tile([P, H, NT, B], F32, name="dist", tag="dist")
            for t in range(NT):
                n = PLANE_COLS[t]
                kq_ps = ps_score.tile([P, B], F32, name="kq_ps", tag="kq")
                nc.tensor.matmul(
                    kq_ps[:, :n],
                    lhsT=qk_t[u][:, B + t * P : B + (t + 1) * P],
                    rhs=qk_t[u][:, t * P : B],
                    start=True,
                    stop=False,
                )
                for i in range(t, NT):
                    nc.tensor.matmul(
                        kq_ps[:, (i - t) * P : (i - t + 1) * P],
                        lhsT=q2_half[u][:, i, 0:1].to_broadcast([P, P]),
                        rhs=ident_f32[:],
                        is_transpose=True,
                        start=False,
                        stop=(i == NT - 1),
                    )
                nc.vector.tensor_scalar(
                    out=dist[g][:, h, t, :n],
                    in0=kq_ps[:, :n],
                    scalar1=k2[u][:, t : t + 1],
                    scalar2=-D2_FLOOR,
                    op0=ALU.subtract,
                    op1=ALU.min,
                )

        def sigmoid_parts(g, quarter):
            if g == S - 1 and quarter == 3:
                return [slice(2, 3), slice(3, 4)]
            return [slice(2 * quarter - 4, 2 * quarter - 2)]

        def activations(g, quarter):
            if quarter < 2:
                if 0:
                    if quarter == 0:
                        return
                    heads = slice(0, H)
                else:
                    heads = slice(2 * quarter, 2 * quarter + 2)
                for t in range(NT):
                    live = dist[g][:, heads, t, : PLANE_COLS[t]]
                    nc.scalar.activation(out=live, in_=live, func=ACT.Ln, scale=-1.0)
                return
            for heads in sigmoid_parts(g, quarter):
                flat = dist[g][:, heads, :, :].rearrange("p h t b -> p h (t b)")
                if 1:
                    nc.scalar.activation(
                        out=first_tile[g % GROUPED_BUFS][:, heads, :],
                        in_=dist[g][:, heads, 0, :P],
                        func=ACT.Sigmoid,
                        scale=-0.5,
                    )
                for i in range(1 if 1 else 0, NT):
                    tiles = flat[:, :, i * P : i * P + (i + 1) * (B - P)].rearrange("p h (t s) -> p h t s", s=B - P)
                    nc.scalar.activation(
                        out=grouped[g % GROUPED_BUFS][:, heads, i * P : (i + 1) * P, : i + 1],
                        in_=tiles[:, :, :, :P].rearrange("p h t j -> p h j t"),
                        func=ACT.Sigmoid,
                        scale=-0.5,
                    )

        def mask_diagonal(u):
            g, h = divmod(u, H)
            first = 1 if 1 else 0
            block = dist[g][:, h, first:, :P]
            nc.gpsimd.affine_select(
                out=block,
                in_=block,
                pattern=[[0, NT - first], [1, P]],
                compare_op=ALU.is_ge,
                fill=MASKED_LN,
                base=0,
                channel_multiplier=-1,
            )

        def place_first_tile(g, heads):
            block = first_tile[g % GROUPED_BUFS][:, heads, :]
            nc.gpsimd.affine_select(
                out=block,
                in_=block,
                pattern=[[0, heads.stop - heads.start], [1, P]],
                compare_op=ALU.is_ge,
                fill=0.0,
                base=0,
                channel_multiplier=-1,
            )
            (nc.vector if 0 else nc.gpsimd).tensor_scalar(
                out=grouped[g % GROUPED_BUFS][:, heads, :P, 0],
                in0=block,
                scalar1=1.0,
                scalar2=0.0,
                op0=ALU.mult,
                op1=ALU.add,
            )

        def quantise_w(u):
            w_codes[u] = work.tile([P, B], U32, name="w_codes", tag="w_codes", bufs=2, align_bytes=64)
            w_scl[u] = work.tile([P, B], U8, name="w_scl", tag="w_scl", bufs=2, align_bytes=64)
            nc.vector.quantize_mx(
                out=w_codes[u][:].bitcast(FP8X4),
                scales=w_scl[u][:],
                in_=grouped[(u // H) % GROUPED_BUFS][:, u % H, :, :].rearrange("p b t -> p (b t)"),
            )

        def attend(u):
            g, h = divmod(u, H)
            o_ps = ps_out.tile([P, NT, P], F32, name="o_ps", tag="o")
            for i in range(NT):
                nc.tensor.matmul_mx(
                    out=o_ps[:, i, :],
                    lhsT=w_codes[u][:, i * P : (i + 1) * P].bitcast(FP8X4),
                    lhsT_scale=w_scl[u][:, i * P : (i + 1) * P],
                    rhs=v_codes[g][:, h * P : (h + 1) * P].bitcast(FP8X4),
                    rhs_scale=v_scl[g][:, h * P : (h + 1) * P],
                    start=True,
                    stop=True,
                )
            o_sb = work.tile([P, NT, P], F32, name="o_sb", tag="o_sb", bufs=3)
            if u % 4 < 4:
                nc.vector.tensor_copy(out=o_sb[:], in_=o_ps[:])
            else:
                nc.scalar.copy(out=o_sb[:], in_=o_ps[:])
            nc.sync.dma_start(out=out[g, :, h * P : (h + 1) * P].rearrange("(i p) n -> p i n", p=P), in_=o_sb[:])

        def transpose_x(g):
            x_grouped = work.tile([P, NT, P, 4], BF16, name="x_grouped", tag="x_grouped", bufs=2, align_bytes=64)
            for pair in range(NT // 2):
                x_ps = ps_prep.tile([P, 2, 2, P], F32, name="x_ps", tag="prep")
                for j in range(2):
                    words = x_rows[g][:, 2 * pair + j, :].bitcast(F32)
                    for u in range(2):
                        nc.tensor.transpose(x_ps[:, j, u, :], words[:, u : DM // 2 : 2], ident_f32[:])
                nc.vector.tensor_copy(
                    out=x_grouped[:].bitcast(F32)[:, 2 * pair : 2 * pair + 2, :, :],
                    in_=x_ps[:].rearrange("p j u c -> p j c u"),
                )
            return x_grouped

        def quantise_x(g, x_grouped):
            x_codes[g] = work.tile([P, B], U32, name="x_codes", tag="x_codes", bufs=2, align_bytes=64)
            x_scl[g] = work.tile([P, B], U8, name="x_scl", tag="x_scl", bufs=2, align_bytes=64)
            nc.vector.quantize_mx(
                out=x_codes[g][:].bitcast(FP8X4),
                scales=x_scl[g][:],
                in_=x_grouped[:].rearrange("p t c v -> p (t c v)"),
            )

        def project_values(u):
            g, h = divmod(u, H)
            v_ps = ps_prep.tile([P, NT, P], F32, name="v_ps", tag="prep")
            for t in range(NT):
                nc.tensor.matmul_mx(
                    out=v_ps[:, t, :],
                    lhsT=x_codes[g][:, t * P : (t + 1) * P].bitcast(FP8X4),
                    lhsT_scale=x_scl[g][:, t * P : (t + 1) * P],
                    rhs=wv_words[:, 4 * h * P : 4 * (h + 1) * P].bitcast(FP8X4),
                    rhs_scale=wv_scl[:, h * P : (h + 1) * P],
                    start=True,
                    stop=True,
                )
            if h == 0:
                v_grouped[g] = work.tile([P, DM, NT], BF16, name="v_grouped", tag="v_grouped", bufs=2, align_bytes=64)
            nc.vector.tensor_tensor(
                out=v_grouped[g][:, h * P : (h + 1) * P, :],
                in0=v_ps[:].rearrange("p t n -> p n t"),
                in1=bias_bc[:, h * P : (h + 1) * P].unsqueeze(2).to_broadcast([P, P, NT]),
                op=ALU.add,
            )

        def quantise_v(g):
            v_codes[g] = work.tile([P, DM], U32, name="v_codes", tag="v_codes", bufs=4, align_bytes=64)
            v_scl[g] = work.tile([P, DM], U8, name="v_scl", tag="v_scl", bufs=4, align_bytes=64)
            nc.vector.quantize_mx(
                out=v_codes[g][:].bitcast(FP8X4),
                scales=v_scl[g][:],
                in_=v_grouped[g][:].rearrange("p n t -> p (n t)"),
            )

        def is_unit(u):
            return 0 <= u < UNITS

        act_at, mask_at, weights_at, sigmoid_tick = {}, {}, {}, {}
        at = 0
        for batch in BATCHES:
            for quarters in ((0, 1), (2, 3)):
                for g in batch:
                    for quarter in quarters:
                        at = max(at + 1, H * g + ACT_BEHIND + quarter) if quarter < 2 else at + 1
                        act_at[at] = (g, quarter)
                        if quarter < 2:
                            mask_at[at + 1 + (0 and quarter == 0)] = H * g + 2 * quarter
                            if 0 and quarter == 1:
                                mask_at[at + 2] = H * g + 2
                        else:
                            sigmoid_tick[(g, quarter - 2)] = at
        at = 0
        for u in range(UNITS):
            at = max(at + 1, sigmoid_tick[(u // H, u % H // 2)] + 2)
            weights_at[at] = u
        last_tick = at + 1
        done_at = dict((u, tick) for tick, u in weights_at.items())
        for g in range(S):
            assert g < GROUPED_BUFS or done_at[H * (g - GROUPED_BUFS) + H - 1] < sigmoid_tick[(g, 0)]
            assert g < 3 or sigmoid_tick[(g - 3, 1)] < H * g
            assert g < 4 or done_at[H * (g - 4) + H - 1] + 1 < H * g + H

        x_waiting = {}
        for tick in range(-max(TRANSPOSE_AHEAD, 9), last_tick + 1):
            if tick in act_at:
                activations(act_at[tick][0], act_at[tick][1])
            if is_unit(tick + NORMS_AHEAD):
                norms(tick + NORMS_AHEAD)
            if is_unit(tick + 9):
                k_norms(tick + 9)
            if tick in (1, 3) and (tick + 1) // 2 < GROUPED_BUFS:
                zero_grouped((tick + 1) // 2)
            if tick in mask_at:
                mask_diagonal(mask_at[tick])
                mask_diagonal(mask_at[tick] + 1)
            if 1 and tick - 1 in act_at and act_at[tick - 1][1] >= 2:
                for heads in sigmoid_parts(act_at[tick - 1][0], act_at[tick - 1][1]):
                    place_first_tile(act_at[tick - 1][0], heads)
            if is_unit(tick):
                scores(tick)
            if tick in weights_at:
                quantise_w(weights_at[tick])
            if is_unit(tick + Q2_AHEAD):
                half_norms(tick + Q2_AHEAD)
            if is_unit(tick):
                project_values(tick)
            if is_unit(tick - H) and tick % H == 0:
                quantise_v(tick // H - 1)
            if tick - 1 in weights_at:
                attend(weights_at[tick - 1])
            if is_unit(tick + TRANSPOSE_AHEAD):
                transpose_qk(tick + TRANSPOSE_AHEAD)
            if is_unit(tick + 2) and (tick + 2) % H == 0:
                x_waiting[(tick + 2) // H] = transpose_x((tick + 2) // H)
            if is_unit(tick + 1) and (tick + 1) % H == 0:
                quantise_x((tick + 1) // H, x_waiting[(tick + 1) // H])
            if is_unit(tick + NORMS_AHEAD) and (tick + NORMS_AHEAD) % H == H - 1:
                if (tick + NORMS_AHEAD) // H + 2 < S:
                    load((tick + NORMS_AHEAD) // H + 2)
                if (tick + NORMS_AHEAD) // H + 3 < S:
                    load_k((tick + NORMS_AHEAD) // H + 3)
